import numpy as np
import ml_dtypes


def mxq(x, axis, fmt="e4m3"):
    dtype, down = {"e4m3": (ml_dtypes.float8_e4m3fn, 7), "e5m2": (ml_dtypes.float8_e5m2, 14)}[fmt]
    v = np.moveaxis(np.asarray(x, np.float32).astype(ml_dtypes.bfloat16).astype(np.float64), axis, -1)
    blocks = v.reshape(v.shape[:-1] + (-1, 32))
    amax = np.abs(blocks).max(-1, keepdims=True)
    byte = np.maximum(np.where(amax > 0, np.frexp(amax)[1] - 1 + 127, 0) - down, 1)
    scale = np.exp2(byte - 127.0)
    codes = (blocks / scale).astype(np.float32).astype(dtype).astype(np.float64)
    return np.moveaxis((codes * scale).reshape(v.shape), -1, axis)


WIDE = False


def mx_kscale(k):
    if not WIDE:
        return np.ones(k)
    levels = np.array([10, -10, 5, -5, 0])
    a = np.random.permutation(np.resize(levels, k // 512 * 4)).reshape(k // 512, 4)
    idx = np.arange(k)
    return np.exp2(a[idx // 512, idx % 128 // 32])


BF16 = ml_dtypes.bfloat16


def bf(x):
    return np.asarray(x, np.float32).astype(BF16)


def f64(x):
    return np.asarray(x).astype(np.float64)


B, LC, LP, D = 8, 256, 768, 512


def setup_inputs():
    s, t = mx_kscale(D), mx_kscale(D)
    return {"comp_feat": bf(np.random.standard_normal((B, LC, D)) * s),
            "prot_feat": bf(np.random.standard_normal((B, LP, D)) * t),
            "W_comp": bf(np.random.standard_normal((D, D)) * 0.3 / np.sqrt(D) / s[None, :]),
            "b_comp": bf(np.random.standard_normal(D) * 0.1),
            "W_prot": bf(np.random.standard_normal((D, D)) * 0.3 / np.sqrt(D) / t[None, :]),
            "b_prot": bf(np.random.standard_normal(D) * 0.1)}


def reference(comp_feat, prot_feat, W_comp, b_comp, W_prot, b_prot):
    comp_trans = np.tanh((mxq(f64(comp_feat), 2, "e4m3") @ mxq(f64(W_comp), 1, "e4m3").T) + f64(b_comp))
    prot_trans = np.tanh((mxq(f64(prot_feat), 2, "e4m3") @ mxq(f64(W_prot), 1, "e4m3").T) + f64(b_prot))
    return mxq(comp_trans, 2, "e4m3") @ mxq(prot_trans, 2, "e4m3").transpose(0, 2, 1)

@@ -1,0 +1,273 @@
+from contextlib import ExitStack
+
+import concourse.mybir as mybir
+from concourse.masks import make_identity
+
+F32 = mybir.dt.float32
+BF16 = mybir.dt.bfloat16
+U32 = mybir.dt.uint32
+U8 = mybir.dt.uint8
+FP8X4 = mybir.dt.float8_e4m3fn_x4
+TANH = mybir.ActivationFunctionType.Tanh
+
+P = 128
+B, LC, LP, D = 8, 256, 768, 512
+GT = 512
+FLOPS = 2 * B * (LC + LP) * D * D + 2 * B * LC * LP * D
+
+PINNED = True
+N_GROUPS = 16
+LAST_SCALAR_B_STEP = 6
+FIRST_VECTOR_O_GROUP = 11
+
+
+def a_list(s):
+    if s == -1:
+        return [0, 1, 2]
+    if s == 0:
+        return [3]
+    if s == 1:
+        return [4, 5]
+    if s == 2:
+        return [6, 7]
+    return [s + 5] if s + 5 <= 17 else []
+
+
+def tile_coattentionlayer_pa_t_kernel(tc, comp_feat, prot_feat, W_comp, b_comp, W_prot, b_prot, out):
+    nc = tc.nc
+    with ExitStack() as ctx:
+        if PINNED:
+            ctx.enter_context(tc.manual_schedule())
+        const = ctx.enter_context(tc.tile_pool(name="const", bufs=1))
+        xin = ctx.enter_context(tc.tile_pool(name="xin", bufs=1))
+        xgp = ctx.enter_context(tc.tile_pool(name="xgp", bufs=3))
+        xqp = ctx.enter_context(tc.tile_pool(name="xqp", bufs=6))
+        tp = ctx.enter_context(tc.tile_pool(name="tp", bufs=3))
+        gp = ctx.enter_context(tc.tile_pool(name="gp", bufs=2))
+        cq = ctx.enter_context(tc.tile_pool(name="cq", bufs=4))
+        pq = ctx.enter_context(tc.tile_pool(name="pq", bufs=4))
+        op = ctx.enter_context(tc.tile_pool(name="op", bufs=4))
+        ps_xt = ctx.enter_context(tc.psum_pool(name="ps_xt", bufs=2))
+        ps_z = ctx.enter_context(tc.psum_pool(name="ps_z", bufs=4))
+        ps_o = ctx.enter_context(tc.psum_pool(name="ps_o", bufs=2))
+
+        prot_flat = prot_feat.flatten_outer_dims()
+        sources = [("w", 0)] + [("c", i) for i in range(4)] + [("w", 1)] + [("p", g) for g in range(12)]
+        groups = [n for n in range(len(sources)) if sources[n][0] != "w"]
+
+        bias_bf = []
+        for w, b_ap in enumerate((b_comp, b_prot)):
+            bt = const.tile([P, 4], BF16, name="bias_bf%d" % w)
+            nc.scalar.dma_start(out=bt[:], in_=b_ap.rearrange("(p j) -> p j", j=4))
+            bias_bf.append(bt)
+
+        warm = const.tile([P, 1], F32, name="warm")
+        nc.vector.memset(warm[:], 0.0)
+        warm2 = const.tile([P, 1], F32, name="warm2")
+        nc.scalar.activation(out=warm2[:], in_=warm[:], func=TANH)
+
+        ident = const.tile([P, P], F32, name="ident")
+        make_identity(nc, ident[:])
+
+        raw = []
+        for n, (kind, i) in enumerate(sources):
+            x = xin.tile([P, 4 * D], BF16, name="x%d" % n)
+            if kind == "w":
+                src = (W_comp, W_prot)[i].rearrange("(p j) k -> p (j k)", j=4)
+                nc.sync.dma_start(out=x[:], in_=src)
+            elif kind == "c":
+                src = comp_feat[2 * i : 2 * i + 2].rearrange("b (p r) k -> p b (r k)", r=2)
+                nc.sync.dma_start(out=x[:].rearrange("p (b f) -> p b f", b=2), in_=src)
+            else:
+                src = prot_flat[GT * i : GT * i + GT, :].rearrange("(t p) k -> p t k", p=P)
+                nc.sync.dma_start(out=x[:].rearrange("p (t k) -> p t k", t=4), in_=src)
+            raw.append(x)
+
+        bias = []
+        for w in range(2):
+            bt = const.tile([P, 4], F32, name="bias%d" % w)
+            nc.vector.tensor_copy(out=bt[:], in_=bias_bf[w][:])
+            bias.append(bt)
+
+        def copy_out(engine, dst, src):
+            if engine == "v":
+                nc.vector.tensor_copy(out=dst, in_=src)
+            else:
+                nc.scalar.copy(out=dst, in_=src)
+
+        xt_of, xg_of, xq_of = {}, {}, {}
+        z_of, th_of, gr_of, tq_of, o_of, out_tiles = {}, {}, {}, {}, {}, {}
+
+        def transposes(n):
+            xf = raw[n][:].bitcast(F32)
+            for h in range(2):
+                xt = ps_xt.tile([P, 512], F32, name="xt", tag="xt")
+                xt_of[(n, h)] = xt
+                for tl in range(2):
+                    for u in range(2):
+                        t = 2 * h + tl
+                        nc.tensor.transpose(
+                            xt[:, (2 * tl + u) * P : (2 * tl + u + 1) * P],
+                            xf[:, 256 * t + P * u : 256 * t + P * u + P],
+                            ident[:],
+                        )
+
+        def copy_source(n, engines):
+            xg = xgp.tile([P, 4 * GT], BF16, name="xg", tag="xg", align_bytes=64)
+            xg_of[n] = xg
+            xgf = xg[:].bitcast(F32)
+            for h in range(2):
+                copy_out(
+                    engines[h],
+                    xgf[:, 512 * h : 512 * h + 512].rearrange("q (t a u) -> q t a u", t=2, u=2),
+                    xt_of[(n, h)][:].rearrange("q (t u a) -> q t a u", t=2, u=2),
+                )
+
+        def quantise_source(n):
+            if sources[n][0] == "w":
+                codes = const.tile([P, GT], U32, name="wc%d" % n, align_bytes=64)
+                scales = const.tile([P, GT], U8, name="ws%d" % n, align_bytes=64)
+            else:
+                codes = xqp.tile([P, GT], U32, name="xc", tag="xc", align_bytes=64)
+                scales = xqp.tile([P, GT], U8, name="xs", tag="xs", align_bytes=64)
+            xq_of[n] = (codes, scales)
+            nc.vector.quantize_mx(out=codes[:].bitcast(FP8X4), scales=scales[:], in_=xg_of[n][:])
+
+        def first_stage(s):
+            n = groups[s]
+            wc, ws = xq_of[0 if sources[n][0] == "c" else 5]
+            xc, xs = xq_of[n]
+            for j in range(4):
+                z = ps_z.tile([P, GT], F32, name="z", tag="z")
+                z_of[(s, j)] = z
+                nc.tensor.matmul_mx(
+                    out=z[:],
+                    lhsT=wc[:, P * j : P * j + P].bitcast(FP8X4),
+                    lhsT_scale=ws[:, P * j : P * j + P],
+                    rhs=xc[:].bitcast(FP8X4),
+                    rhs_scale=xs[:],
+                    start=True,
+                    stop=True,
+                )
+
+        def tanh(s):
+            w = 0 if sources[groups[s]][0] == "c" else 1
+            th = tp.tile([P, 4 * GT], BF16, name="th", tag="th")
+            th_of[s] = th
+            for j in range(4):
+                nc.scalar.activation(
+                    out=th[:, GT * j : GT * j + GT],
+                    in_=z_of[(s, j)][:],
+                    func=TANH,
+                    bias=bias[w][:, j : j + 1],
+                    scale=1.0,
+                )
+
+        def regroup(s):
+            gr = gp.tile([P, 4 * GT], BF16, name="gr", tag="gr", align_bytes=64)
+            gr_of[s] = gr
+            nc.vector.tensor_copy(
+                out=gr[:].rearrange("p (c i j) -> p c j i", i=4, j=4),
+                in_=th_of[s][:].rearrange("p (j c i) -> p c j i", j=4, i=4),
+            )
+
+        def quantise_trans(s):
+            pool = cq if sources[groups[s]][0] == "c" else pq
+            tcd = pool.tile([P, GT], U32, name="tcd", tag="tcd", align_bytes=64)
+            tsc = pool.tile([P, GT], U8, name="tsc", tag="tsc", align_bytes=64)
+            tq_of[s] = (tcd, tsc)
+            nc.vector.quantize_mx(out=tcd[:].bitcast(FP8X4), scales=tsc[:], in_=gr_of[s][:])
+
+        def units_of(g):
+            i, part = g // 3, g % 3
+            if part == 0:
+                return [(2 * i, r, 0, 512, 0) for r in range(2)]
+            if part == 2:
+                return [(2 * i + 1, r, 0, 512, 256) for r in range(2)]
+            return [(2 * i, None, 0, 256, 512), (2 * i + 1, None, 256, 256, 0)]
+
+        def second_stage(s):
+            g = sources[groups[s]][1]
+            c_codes, c_scales = tq_of[g // 3]
+            p_codes, p_scales = tq_of[s]
+            for un, (b, r, c0, width, n0) in enumerate(units_of(g)):
+                o = ps_o.tile([P, 512], F32, name="o", tag="o")
+                o_of[(s, un)] = o
+                rs = [r] if r is not None else [0, 1]
+                for q, rr in enumerate(rs):
+                    m0 = 256 * (b % 2) + P * rr
+                    nc.tensor.matmul_mx(
+                        out=o[:, q * width : (q + 1) * width],
+                        lhsT=c_codes[:, m0 : m0 + P].bitcast(FP8X4),
+                        lhsT_scale=c_scales[:, m0 : m0 + P],
+                        rhs=p_codes[:, c0 : c0 + width].bitcast(FP8X4),
+                        rhs_scale=p_scales[:, c0 : c0 + width],
+                        start=True,
+                        stop=True,
+                    )
+
+        def affinity_out(s, un, engine):
+            g = sources[groups[s]][1]
+            b, r, c0, width, n0 = units_of(g)[un]
+            if b not in out_tiles:
+                ot_new = op.tile([P, 2 * LP], F32, name="ot", tag="ot")
+                out_tiles[b] = ot_new
+            ot = out_tiles[b]
+            o = o_of[(s, un)]
+            if r is not None:
+                copy_out(engine, ot[:, LP * r + n0 : LP * r + n0 + 512], o[:])
+            else:
+                copy_out(
+                    engine,
+                    ot[:].rearrange("p (r n) -> p r n", r=2)[:, :, n0 : n0 + 256],
+                    o[:].rearrange("p (r n) -> p r n", r=2),
+                )
+
+        def stores(s):
+            g = sources[groups[s]][1]
+            i, part = g // 3, g % 3
+            for b in {0: [], 1: [2 * i], 2: [2 * i + 1]}[part]:
+                nc.sync.dma_start(out=out[b].rearrange("(a r) n -> a (r n)", r=2), in_=out_tiles[b][:])
+
+        def o_engine(s, un):
+            return "v" if (s >= FIRST_VECTOR_O_GROUP and un == 0) else "s"
+
+        copied = []
+        for s in range(-1, N_GROUPS + 2):
+            b_engines = "vs" if s <= LAST_SCALAR_B_STEP else "vv"
+            if s == -1:
+                for n in a_list(s):
+                    transposes(n)
+                    copy_source(n, b_engines)
+                    quantise_source(n)
+                first_stage(0)
+                continue
+            s2 = s - 2
+            has_s2 = 4 <= s2 < N_GROUPS
+            if has_s2:
+                second_stage(s2)
+            for n in a_list(s):
+                transposes(n)
+            if 0 <= s - 1 < N_GROUPS:
+                regroup(s - 1)
+            for n in copied:
+                quantise_source(n)
+            copied = []
+            if s + 1 < N_GROUPS:
+                first_stage(s + 1)
+            if s < N_GROUPS:
+                tanh(s)
+            if has_s2:
+                for un in range(2):
+                    if o_engine(s2, un) == "s":
+                        affinity_out(s2, un, "s")
+            for n in a_list(s):
+                copy_source(n, b_engines)
+                copied.append(n)
+            if 0 <= s - 1 < N_GROUPS:
+                quantise_trans(s - 1)
+            if has_s2:
+                for un in range(2):
+                    if o_engine(s2, un) == "v":
+                        affinity_out(s2, un, "v")
+                stores(s2)

@@ -12,39 +12,53 @@ TANH = mybir.ActivationFunctionType.Tanh
 
 P = 128
 B, LC, LP, D = 8, 256, 768, 512
-GT = 512
 FLOPS = 2 * B * (LC + LP) * D * D + 2 * B * LC * LP * D
 
-PINNED = True
-N_GROUPS = 16
+LEAD = 3
 LAST_SCALAR_B_STEP = 6
-FIRST_VECTOR_O_GROUP = 11
+FIRST_VECTOR_O_GROUP = 12
+LAST_RAMP_SOURCE = 9
+
+SOURCES = (
+    [("w", (0, 0), 256), ("c", 0, 256), ("w", (0, 1), 256), ("c", 1, 256)]
+    + [("c", b, 512) for b in (2, 4, 6)]
+    + [("w", (1, None), 512)]
+    + [("p", 512 * i, 512) for i in range(11)]
+    + [("p", 5632, 256), ("p", 5888, 256)]
+)
+GROUPS = [n for n in range(len(SOURCES)) if SOURCES[n][0] != "w"]
+N_GROUPS = len(GROUPS)
 
 
-def a_list(s):
-    if s == -1:
-        return [0, 1, 2]
-    if s == 0:
-        return [3]
-    if s == 1:
-        return [4, 5]
-    if s == 2:
-        return [6, 7]
-    return [s + 5] if s + 5 <= 17 else []
+def units_of(g):
+    kind, t0, width = SOURCES[GROUPS[g]]
+    if kind != "p":
+        return []
+    units = []
+    t = t0
+    while t < t0 + width:
+        b = t // LP
+        end = min(t0 + width, (b + 1) * LP)
+        if end - t == 512:
+            units.append((b, [0], t - t0, 512, t - LP * b))
+            units.append((b, [1], t - t0, 512, t - LP * b))
+        else:
+            units.append((b, [0, 1], t - t0, end - t, t - LP * b))
+        t = end
+    return units
 
 
 def tile_coattentionlayer_pa_t_kernel(tc, comp_feat, prot_feat, W_comp, b_comp, W_prot, b_prot, out):
     nc = tc.nc
     with ExitStack() as ctx:
-        if PINNED:
-            ctx.enter_context(tc.manual_schedule())
+        ctx.enter_context(tc.manual_schedule())
         const = ctx.enter_context(tc.tile_pool(name="const", bufs=1))
         xin = ctx.enter_context(tc.tile_pool(name="xin", bufs=1))
         xgp = ctx.enter_context(tc.tile_pool(name="xgp", bufs=3))
         xqp = ctx.enter_context(tc.tile_pool(name="xqp", bufs=6))
         tp = ctx.enter_context(tc.tile_pool(name="tp", bufs=3))
         gp = ctx.enter_context(tc.tile_pool(name="gp", bufs=2))
-        cq = ctx.enter_context(tc.tile_pool(name="cq", bufs=4))
+        cq = ctx.enter_context(tc.tile_pool(name="cq", bufs=5))
         pq = ctx.enter_context(tc.tile_pool(name="pq", bufs=4))
         op = ctx.enter_context(tc.tile_pool(name="op", bufs=4))
         ps_xt = ctx.enter_context(tc.psum_pool(name="ps_xt", bufs=2))
@@ -52,8 +66,6 @@ def tile_coattentionlayer_pa_t_kernel(tc, comp_feat, prot_feat, W_comp, b_comp, 
         ps_o = ctx.enter_context(tc.psum_pool(name="ps_o", bufs=2))
 
         prot_flat = prot_feat.flatten_outer_dims()
-        sources = [("w", 0)] + [("c", i) for i in range(4)] + [("w", 1)] + [("p", g) for g in range(12)]
-        groups = [n for n in range(len(sources)) if sources[n][0] != "w"]
 
         bias_bf = []
         for w, b_ap in enumerate((b_comp, b_prot)):
@@ -70,17 +82,19 @@ def tile_coattentionlayer_pa_t_kernel(tc, comp_feat, prot_feat, W_comp, b_comp, 
         make_identity(nc, ident[:])
 
         raw = []
-        for n, (kind, i) in enumerate(sources):
-            x = xin.tile([P, 4 * D], BF16, name="x%d" % n)
+        for n, (kind, i, width) in enumerate(SOURCES):
+            x = xin.tile([P, 4 * width], BF16, name="x%d" % n)
             if kind == "w":
-                src = (W_comp, W_prot)[i].rearrange("(p j) k -> p (j k)", j=4)
-                nc.sync.dma_start(out=x[:], in_=src)
+                w_ap = (W_comp, W_prot)[i[0]].rearrange("(p j) k -> p j k", j=4)
+                if i[1] is not None:
+                    w_ap = w_ap[:, 2 * i[1] : 2 * i[1] + 2, :]
+                nc.sync.dma_start(out=x[:].rearrange("p (j k) -> p j k", k=D), in_=w_ap)
             elif kind == "c":
-                src = comp_feat[2 * i : 2 * i + 2].rearrange("b (p r) k -> p b (r k)", r=2)
-                nc.sync.dma_start(out=x[:].rearrange("p (b f) -> p b f", b=2), in_=src)
+                src = comp_feat[i : i + width // LC].rearrange("b (p r) k -> p b (r k)", r=2)
+                nc.sync.dma_start(out=x[:].rearrange("p (b f) -> p b f", f=2 * D), in_=src)
             else:
-                src = prot_flat[GT * i : GT * i + GT, :].rearrange("(t p) k -> p t k", p=P)
-                nc.sync.dma_start(out=x[:].rearrange("p (t k) -> p t k", t=4), in_=src)
+                src = prot_flat[i : i + width, :].rearrange("(t p) k -> p t k", p=P)
+                nc.sync.dma_start(out=x[:].rearrange("p (t k) -> p t k", k=D), in_=src)
             raw.append(x)
 
         bias = []
@@ -95,13 +109,18 @@ def tile_coattentionlayer_pa_t_kernel(tc, comp_feat, prot_feat, W_comp, b_comp, 
             else:
                 nc.scalar.copy(out=dst, in_=src)
 
-        xt_of, xg_of, xq_of = {}, {}, {}
-        z_of, th_of, gr_of, tq_of, o_of, out_tiles = {}, {}, {}, {}, {}, {}
+        xt_of, xg_of, xq_of, w_q = {}, {}, {}, {}
+        z_of, th_of, gr_of, tq_of, comp_q, o_of, out_tiles = {}, {}, {}, {}, {}, {}, {}
+        ramp_banks = []
 
         def transposes(n):
             xf = raw[n][:].bitcast(F32)
-            for h in range(2):
-                xt = ps_xt.tile([P, 512], F32, name="xt", tag="xt")
+            for h in range(SOURCES[n][2] // 256):
+                if n <= LAST_RAMP_SOURCE and len(ramp_banks) % 2 == 1:
+                    xt = ps_o.tile([P, 512], F32, name="o", tag="o")
+                else:
+                    xt = ps_xt.tile([P, 512], F32, name="xt", tag="xt")
+                ramp_banks.append(n)
                 xt_of[(n, h)] = xt
                 for tl in range(2):
                     for u in range(2):
@@ -112,90 +131,90 @@ def tile_coattentionlayer_pa_t_kernel(tc, comp_feat, prot_feat, W_comp, b_comp, 
                             ident[:],
                         )
 
-        def copy_source(n, engines):
-            xg = xgp.tile([P, 4 * GT], BF16, name="xg", tag="xg", align_bytes=64)
-            xg_of[n] = xg
-            xgf = xg[:].bitcast(F32)
-            for h in range(2):
-                copy_out(
-                    engines[h],
-                    xgf[:, 512 * h : 512 * h + 512].rearrange("q (t a u) -> q t a u", t=2, u=2),
-                    xt_of[(n, h)][:].rearrange("q (t u a) -> q t a u", t=2, u=2),
-                )
+        def copy_source(n, h, engine):
+            if n not in xg_of:
+                xg_new = xgp.tile([P, 4 * SOURCES[n][2]], BF16, name="xg", tag="xg", align_bytes=64)
+                xg_of[n] = xg_new
+            xgf = xg_of[n][:].bitcast(F32)
+            copy_out(
+                engine,
+                xgf[:, 512 * h : 512 * h + 512].rearrange("q (t a u) -> q t a u", t=2, u=2),
+                xt_of[(n, h)][:].rearrange("q (t u a) -> q t a u", t=2, u=2),
+            )
 
         def quantise_source(n):
-            if sources[n][0] == "w":
-                codes = const.tile([P, GT], U32, name="wc%d" % n, align_bytes=64)
-                scales = const.tile([P, GT], U8, name="ws%d" % n, align_bytes=64)
+            kind, i, width = SOURCES[n]
+            if kind == "w":
+                codes = const.tile([P, width], U32, name="wc%d" % n, align_bytes=64)
+                scales = const.tile([P, width], U8, name="ws%d" % n, align_bytes=64)
+                first_j = 0 if i[1] is None else 2 * i[1]
+                for jj in range(width // P):
+                    w_q[(i[0], first_j + jj)] = (codes[:, P * jj : P * jj + P], scales[:, P * jj : P * jj + P])
             else:
-                codes = xqp.tile([P, GT], U32, name="xc", tag="xc", align_bytes=64)
-                scales = xqp.tile([P, GT], U8, name="xs", tag="xs", align_bytes=64)
-            xq_of[n] = (codes, scales)
+                codes = xqp.tile([P, width], U32, name="xc", tag="xc", align_bytes=64)
+                scales = xqp.tile([P, width], U8, name="xs", tag="xs", align_bytes=64)
+                xq_of[n] = (codes, scales)
             nc.vector.quantize_mx(out=codes[:].bitcast(FP8X4), scales=scales[:], in_=xg_of[n][:])
 
-        def first_stage(s):
-            n = groups[s]
-            wc, ws = xq_of[0 if sources[n][0] == "c" else 5]
+        def first_stage(g):
+            n = GROUPS[g]
+            kind, i, width = SOURCES[n]
             xc, xs = xq_of[n]
             for j in range(4):
-                z = ps_z.tile([P, GT], F32, name="z", tag="z")
-                z_of[(s, j)] = z
+                wc, ws = w_q[(0 if kind == "c" else 1, j)]
+                z = ps_z.tile([P, 512], F32, name="z", tag="z")
+                z_of[(g, j)] = z
                 nc.tensor.matmul_mx(
-                    out=z[:],
-                    lhsT=wc[:, P * j : P * j + P].bitcast(FP8X4),
-                    lhsT_scale=ws[:, P * j : P * j + P],
+                    out=z[:, :width],
+                    lhsT=wc.bitcast(FP8X4),
+                    lhsT_scale=ws,
                     rhs=xc[:].bitcast(FP8X4),
                     rhs_scale=xs[:],
                     start=True,
                     stop=True,
                 )
 
-        def tanh(s):
-            w = 0 if sources[groups[s]][0] == "c" else 1
-            th = tp.tile([P, 4 * GT], BF16, name="th", tag="th")
-            th_of[s] = th
+        def tanh(g):
+            kind, i, width = SOURCES[GROUPS[g]]
+            th = tp.tile([P, 4 * width], BF16, name="th", tag="th")
+            th_of[g] = th
             for j in range(4):
                 nc.scalar.activation(
-                    out=th[:, GT * j : GT * j + GT],
-                    in_=z_of[(s, j)][:],
+                    out=th[:, width * j : width * j + width],
+                    in_=z_of[(g, j)][:, :width],
                     func=TANH,
-                    bias=bias[w][:, j : j + 1],
+                    bias=bias[0 if kind == "c" else 1][:, j : j + 1],
                     scale=1.0,
                 )
 
-        def regroup(s):
-            gr = gp.tile([P, 4 * GT], BF16, name="gr", tag="gr", align_bytes=64)
-            gr_of[s] = gr
+        def regroup(g):
+            width = SOURCES[GROUPS[g]][2]
+            gr = gp.tile([P, 4 * width], BF16, name="gr", tag="gr", align_bytes=64)
+            gr_of[g] = gr
             nc.vector.tensor_copy(
                 out=gr[:].rearrange("p (c i j) -> p c j i", i=4, j=4),
-                in_=th_of[s][:].rearrange("p (j c i) -> p c j i", j=4, i=4),
+                in_=th_of[g][:].rearrange("p (j c i) -> p c j i", j=4, i=4),
             )
 
-        def quantise_trans(s):
-            pool = cq if sources[groups[s]][0] == "c" else pq
-            tcd = pool.tile([P, GT], U32, name="tcd", tag="tcd", align_bytes=64)
-            tsc = pool.tile([P, GT], U8, name="tsc", tag="tsc", align_bytes=64)
-            tq_of[s] = (tcd, tsc)
-            nc.vector.quantize_mx(out=tcd[:].bitcast(FP8X4), scales=tsc[:], in_=gr_of[s][:])
+        def quantise_trans(g):
+            kind, i, width = SOURCES[GROUPS[g]]
+            pool = cq if kind == "c" else pq
+            tcd = pool.tile([P, width], U32, name="tcd", tag="tcd", align_bytes=64)
+            tsc = pool.tile([P, width], U8, name="tsc", tag="tsc", align_bytes=64)
+            tq_of[g] = (tcd, tsc)
+            if kind == "c":
+                for bb in range(width // LC):
+                    comp_q[i + bb] = (tcd, tsc, LC * bb)
+            nc.vector.quantize_mx(out=tcd[:].bitcast(FP8X4), scales=tsc[:], in_=gr_of[g][:])
 
-        def units_of(g):
-            i, part = g // 3, g % 3
-            if part == 0:
-                return [(2 * i, r, 0, 512, 0) for r in range(2)]
-            if part == 2:
-                return [(2 * i + 1, r, 0, 512, 256) for r in range(2)]
-            return [(2 * i, None, 0, 256, 512), (2 * i + 1, None, 256, 256, 0)]
-
-        def second_stage(s):
-            g = sources[groups[s]][1]
-            c_codes, c_scales = tq_of[g // 3]
-            p_codes, p_scales = tq_of[s]
-            for un, (b, r, c0, width, n0) in enumerate(units_of(g)):
+        def second_stage(g):
+            p_codes, p_scales = tq_of[g]
+            for un, (b, rs, c0, width, n0) in enumerate(units_of(g)):
+                c_codes, c_scales, off = comp_q[b]
                 o = ps_o.tile([P, 512], F32, name="o", tag="o")
-                o_of[(s, un)] = o
-                rs = [r] if r is not None else [0, 1]
-                for q, rr in enumerate(rs):
-                    m0 = 256 * (b % 2) + P * rr
+                o_of[(g, un)] = o
+                for q, r in enumerate(rs):
+                    m0 = off + P * r
                     nc.tensor.matmul_mx(
                         out=o[:, q * width : (q + 1) * width],
                         lhsT=c_codes[:, m0 : m0 + P].bitcast(FP8X4),
@@ -206,48 +225,62 @@ def tile_coattentionlayer_pa_t_kernel(tc, comp_feat, prot_feat, W_comp, b_comp, 
                         stop=True,
                     )
 
-        def affinity_out(s, un, engine):
-            g = sources[groups[s]][1]
-            b, r, c0, width, n0 = units_of(g)[un]
+        def affinity_out(g, un, engine):
+            b, rs, c0, width, n0 = units_of(g)[un]
             if b not in out_tiles:
                 ot_new = op.tile([P, 2 * LP], F32, name="ot", tag="ot")
                 out_tiles[b] = ot_new
             ot = out_tiles[b]
-            o = o_of[(s, un)]
-            if r is not None:
-                copy_out(engine, ot[:, LP * r + n0 : LP * r + n0 + 512], o[:])
+            o = o_of[(g, un)]
+            if len(rs) == 1:
+                copy_out(engine, ot[:, LP * rs[0] + n0 : LP * rs[0] + n0 + width], o[:])
             else:
                 copy_out(
                     engine,
-                    ot[:].rearrange("p (r n) -> p r n", r=2)[:, :, n0 : n0 + 256],
+                    ot[:].rearrange("p (r n) -> p r n", r=2)[:, :, n0 : n0 + width],
                     o[:].rearrange("p (r n) -> p r n", r=2),
                 )
 
-        def stores(s):
-            g = sources[groups[s]][1]
-            i, part = g // 3, g % 3
-            for b in {0: [], 1: [2 * i], 2: [2 * i + 1]}[part]:
-                nc.sync.dma_start(out=out[b].rearrange("(a r) n -> a (r n)", r=2), in_=out_tiles[b][:])
+        def stores(g):
+            done = []
+            for b, rs, c0, width, n0 in units_of(g):
+                if b == B - 1:
+                    if (b, n0, n0 + width) not in done:
+                        done.append((b, n0, n0 + width))
+                elif n0 + width == LP and (b, 0, LP) not in done:
+                    done.append((b, 0, LP))
+            for b, n0, n1 in done:
+                nc.sync.dma_start(
+                    out=out[b].rearrange("(a r) n -> a r n", r=2)[:, :, n0:n1],
+                    in_=out_tiles[b][:].rearrange("p (r n) -> p r n", r=2)[:, :, n0:n1],
+                )
 
-        def o_engine(s, un):
-            return "v" if (s >= FIRST_VECTOR_O_GROUP and un == 0) else "s"
+        def o_engine(g, un):
+            return "v" if (g >= FIRST_VECTOR_O_GROUP and un == 0) else "s"
 
-        copied = []
-        for s in range(-1, N_GROUPS + 2):
-            b_engines = "vs" if s <= LAST_SCALAR_B_STEP else "vv"
-            if s == -1:
-                for n in a_list(s):
-                    transposes(n)
-                    copy_source(n, b_engines)
-                    quantise_source(n)
-                first_stage(0)
-                continue
-            s2 = s - 2
-            has_s2 = 4 <= s2 < N_GROUPS
-            if has_s2:
-                second_stage(s2)
-            for n in a_list(s):
+        for n, engine in ((0, "v"), (1, "s"), (2, "v"), (3, "s")):
+            transposes(n)
+            copy_source(n, 0, engine)
+            quantise_source(n)
+        transposes(4)
+        copy_source(4, 0, "v")
+        copy_source(4, 1, "s")
+        first_stage(0)
+        copied = [4]
+        next_source = 5
+
+        for s in range(N_GROUPS + 3):
+            new = []
+            target = GROUPS[min(N_GROUPS - 1, s + LEAD)] if s < N_GROUPS else len(SOURCES) - 1
+            while next_source <= target and len(new) < 2:
+                new.append(next_source)
+                next_source += 1
+            g2 = s - 2
+            n_units = len(units_of(g2)) if 0 <= g2 < N_GROUPS else 0
+            for n in new:
                 transposes(n)
+            if n_units:
+                second_stage(g2)
             if 0 <= s - 1 < N_GROUPS:
                 regroup(s - 1)
             for n in copied:
@@ -257,17 +290,19 @@ def tile_coattentionlayer_pa_t_kernel(tc, comp_feat, prot_feat, W_comp, b_comp, 
                 first_stage(s + 1)
             if s < N_GROUPS:
                 tanh(s)
-            if has_s2:
-                for un in range(2):
-                    if o_engine(s2, un) == "s":
-                        affinity_out(s2, un, "s")
-            for n in a_list(s):
-                copy_source(n, b_engines)
-                copied.append(n)
+            for un in range(n_units):
+                if o_engine(g2, un) == "s":
+                    affinity_out(g2, un, "s")
+            for engine in "vs":
+                for n in new:
+                    for h in range(SOURCES[n][2] // 256):
+                        if ("s" if (s <= LAST_SCALAR_B_STEP and h == 1) else "v") == engine:
+                            copy_source(n, h, engine)
+            copied = list(new)
             if 0 <= s - 1 < N_GROUPS:
                 quantise_trans(s - 1)
-            if has_s2:
-                for un in range(2):
-                    if o_engine(s2, un) == "v":
-                        affinity_out(s2, un, "v")
-                stores(s2)
+            for un in range(n_units):
+                if o_engine(g2, un) == "v":
+                    affinity_out(g2, un, "v")
+            if n_units:
+                stores(g2)

@@ -15,8 +15,8 @@ B, LC, LP, D = 8, 256, 768, 512
 FLOPS = 2 * B * (LC + LP) * D * D + 2 * B * LC * LP * D
 
 LEAD = 3
-LAST_SCALAR_B_STEP = 6
-FIRST_VECTOR_O_GROUP = 12
+LAST_SCALAR_B_STEP = 7
+FIRST_VECTOR_O_GROUP = 13
 LAST_RAMP_SOURCE = 9
 
 SOURCES = (

@@ -15,8 +15,9 @@ B, LC, LP, D = 8, 256, 768, 512
 FLOPS = 2 * B * (LC + LP) * D * D + 2 * B * LC * LP * D
 
 LEAD = 3
-LAST_SCALAR_B_STEP = 7
+LAST_SCALAR_B_STEP = 8
 FIRST_VECTOR_O_GROUP = 13
+LAST_VECTOR_O_GROUP = 14
 LAST_RAMP_SOURCE = 9
 
 SOURCES = (
@@ -256,7 +257,7 @@ def tile_coattentionlayer_pa_t_kernel(tc, comp_feat, prot_feat, W_comp, b_comp, 
                 )
 
         def o_engine(g, un):
-            return "v" if (g >= FIRST_VECTOR_O_GROUP and un == 0) else "s"
+            return "v" if (FIRST_VECTOR_O_GROUP <= g <= LAST_VECTOR_O_GROUP and un == 0) else "s"
 
         for n, engine in ((0, "v"), (1, "s"), (2, "v"), (3, "s")):
             transposes(n)

@@ -8,6 +8,8 @@ BF16 = mybir.dt.bfloat16
 U32 = mybir.dt.uint32
 U8 = mybir.dt.uint8
 FP8X4 = mybir.dt.float8_e4m3fn_x4
+MULT = mybir.AluOpType.mult
+ADD = mybir.AluOpType.add
 TANH = mybir.ActivationFunctionType.Tanh
 
 P = 128
@@ -15,13 +17,21 @@ B, LC, LP, D = 8, 256, 768, 512
 FLOPS = 2 * B * (LC + LP) * D * D + 2 * B * LC * LP * D
 
 LEAD = 3
-LAST_SCALAR_B_STEP = 8
-FIRST_VECTOR_O_GROUP = 13
-LAST_VECTOR_O_GROUP = 14
-LAST_RAMP_SOURCE = 9
+WIDE_FROM = 13
+GPB = 1
+TAIL = 18
+FINE_FROM = 14
+AFF_LAG = 3
+EXTRA = (6,9,12,14,17)
+GP_TOKENS = 192
+GP_FIRST = 2
+GP_LAST = 14
+WARM_MATMULS = 3
+LAST_SCALAR_B_STEP = 7
+LAST_RAMP_SOURCE = 11
 
 SOURCES = (
-    [("w", (0, 0), 256), ("c", 0, 256), ("w", (0, 1), 256), ("c", 1, 256)]
+    [("w", (0, 0), 128), ("c", 0, 256), ("w", (0, 1), 128), ("w", (0, 2), 128), ("w", (0, 3), 128), ("c", 1, 256)]
     + [("c", b, 512) for b in (2, 4, 6)]
     + [("w", (1, None), 512)]
     + [("p", 512 * i, 512) for i in range(11)]
@@ -40,9 +50,9 @@ def units_of(g):
     while t < t0 + width:
         b = t // LP
         end = min(t0 + width, (b + 1) * LP)
-        if end - t == 512:
-            units.append((b, [0], t - t0, 512, t - LP * b))
-            units.append((b, [1], t - t0, 512, t - LP * b))
+        if end - t == 512 or g == N_GROUPS - 1:
+            units.append((b, [0], t - t0, end - t, t - LP * b))
+            units.append((b, [1], t - t0, end - t, t - LP * b))
         else:
             units.append((b, [0, 1], t - t0, end - t, t - LP * b))
         t = end
@@ -55,12 +65,12 @@ def tile_coattentionlayer_pa_t_kernel(tc, comp_feat, prot_feat, W_comp, b_comp, 
         ctx.enter_context(tc.manual_schedule())
         const = ctx.enter_context(tc.tile_pool(name="const", bufs=1))
         xin = ctx.enter_context(tc.tile_pool(name="xin", bufs=1))
-        xgp = ctx.enter_context(tc.tile_pool(name="xgp", bufs=3))
+        xgp = ctx.enter_context(tc.tile_pool(name="xgp", bufs=6))
         xqp = ctx.enter_context(tc.tile_pool(name="xqp", bufs=6))
         tp = ctx.enter_context(tc.tile_pool(name="tp", bufs=3))
-        gp = ctx.enter_context(tc.tile_pool(name="gp", bufs=2))
+        gp = ctx.enter_context(tc.tile_pool(name="gp", bufs=GPB))
         cq = ctx.enter_context(tc.tile_pool(name="cq", bufs=5))
-        pq = ctx.enter_context(tc.tile_pool(name="pq", bufs=4))
+        pq = ctx.enter_context(tc.tile_pool(name="pq", bufs=5))
         op = ctx.enter_context(tc.tile_pool(name="op", bufs=4))
         ps_xt = ctx.enter_context(tc.psum_pool(name="ps_xt", bufs=2))
         ps_z = ctx.enter_context(tc.psum_pool(name="ps_z", bufs=4))
@@ -68,16 +78,22 @@ def tile_coattentionlayer_pa_t_kernel(tc, comp_feat, prot_feat, W_comp, b_comp, 
 
         prot_flat = prot_feat.flatten_outer_dims()
 
-        bias_bf = []
+        bias = []
         for w, b_ap in enumerate((b_comp, b_prot)):
-            bt = const.tile([P, 4], BF16, name="bias_bf%d" % w)
+            bt = const.tile([P, 4], BF16, name="bias%d" % w)
             nc.scalar.dma_start(out=bt[:], in_=b_ap.rearrange("(p j) -> p j", j=4))
-            bias_bf.append(bt)
+            bias.append(bt)
 
         warm = const.tile([P, 1], F32, name="warm")
         nc.vector.memset(warm[:], 0.0)
         warm2 = const.tile([P, 1], F32, name="warm2")
         nc.scalar.activation(out=warm2[:], in_=warm[:], func=TANH)
+
+        dummy = const.tile([P, 512], BF16, name="dummy")
+        nc.vector.memset(dummy[:], 0.0)
+        for i in range(WARM_MATMULS):
+            wz = ps_z.tile([P, 512], F32, name="z", tag="z")
+            nc.tensor.matmul(wz[:], lhsT=dummy[:, :P], rhs=dummy[:], start=True, stop=True)
 
         ident = const.tile([P, P], F32, name="ident")
         make_identity(nc, ident[:])
@@ -88,7 +104,7 @@ def tile_coattentionlayer_pa_t_kernel(tc, comp_feat, prot_feat, W_comp, b_comp, 
             if kind == "w":
                 w_ap = (W_comp, W_prot)[i[0]].rearrange("(p j) k -> p j k", j=4)
                 if i[1] is not None:
-                    w_ap = w_ap[:, 2 * i[1] : 2 * i[1] + 2, :]
+                    w_ap = w_ap[:, i[1] : i[1] + 1, :]
                 nc.sync.dma_start(out=x[:].rearrange("p (j k) -> p j k", k=D), in_=w_ap)
             elif kind == "c":
                 src = comp_feat[i : i + width // LC].rearrange("b (p r) k -> p b (r k)", r=2)
@@ -97,12 +113,6 @@ def tile_coattentionlayer_pa_t_kernel(tc, comp_feat, prot_feat, W_comp, b_comp, 
                 src = prot_flat[i : i + width, :].rearrange("(t p) k -> p t k", p=P)
                 nc.sync.dma_start(out=x[:].rearrange("p (t k) -> p t k", k=D), in_=src)
             raw.append(x)
-
-        bias = []
-        for w in range(2):
-            bt = const.tile([P, 4], F32, name="bias%d" % w)
-            nc.vector.tensor_copy(out=bt[:], in_=bias_bf[w][:])
-            bias.append(bt)
 
         def copy_out(engine, dst, src):
             if engine == "v":
@@ -114,18 +124,24 @@ def tile_coattentionlayer_pa_t_kernel(tc, comp_feat, prot_feat, W_comp, b_comp, 
         z_of, th_of, gr_of, tq_of, comp_q, o_of, out_tiles = {}, {}, {}, {}, {}, {}, {}
         ramp_banks = []
 
+        def tiles_of(n):
+            return 1 if SOURCES[n][2] <= 256 and n < 6 else 2
+
+        def banks_of(n):
+            return range(SOURCES[n][2] // (P * tiles_of(n)))
+
         def transposes(n):
             xf = raw[n][:].bitcast(F32)
-            for h in range(SOURCES[n][2] // 256):
+            for h in banks_of(n):
                 if n <= LAST_RAMP_SOURCE and len(ramp_banks) % 2 == 1:
                     xt = ps_o.tile([P, 512], F32, name="o", tag="o")
                 else:
                     xt = ps_xt.tile([P, 512], F32, name="xt", tag="xt")
                 ramp_banks.append(n)
                 xt_of[(n, h)] = xt
-                for tl in range(2):
+                for tl in range(tiles_of(n)):
                     for u in range(2):
-                        t = 2 * h + tl
+                        t = tiles_of(n) * h + tl
                         nc.tensor.transpose(
                             xt[:, (2 * tl + u) * P : (2 * tl + u + 1) * P],
                             xf[:, 256 * t + P * u : 256 * t + P * u + P],
@@ -137,10 +153,11 @@ def tile_coattentionlayer_pa_t_kernel(tc, comp_feat, prot_feat, W_comp, b_comp, 
                 xg_new = xgp.tile([P, 4 * SOURCES[n][2]], BF16, name="xg", tag="xg", align_bytes=64)
                 xg_of[n] = xg_new
             xgf = xg_of[n][:].bitcast(F32)
+            nt = tiles_of(n)
             copy_out(
                 engine,
-                xgf[:, 512 * h : 512 * h + 512].rearrange("q (t a u) -> q t a u", t=2, u=2),
-                xt_of[(n, h)][:].rearrange("q (t u a) -> q t a u", t=2, u=2),
+                xgf[:, 256 * nt * h : 256 * nt * (h + 1)].rearrange("q (t a u) -> q t a u", t=nt, u=2),
+                xt_of[(n, h)][:, : 256 * nt].rearrange("q (t u a) -> q t a u", t=nt, u=2),
             )
 
         def quantise_source(n):
@@ -148,7 +165,7 @@ def tile_coattentionlayer_pa_t_kernel(tc, comp_feat, prot_feat, W_comp, b_comp, 
             if kind == "w":
                 codes = const.tile([P, width], U32, name="wc%d" % n, align_bytes=64)
                 scales = const.tile([P, width], U8, name="ws%d" % n, align_bytes=64)
-                first_j = 0 if i[1] is None else 2 * i[1]
+                first_j = 0 if i[1] is None else i[1]
                 for jj in range(width // P):
                     w_q[(i[0], first_j + jj)] = (codes[:, P * jj : P * jj + P], scales[:, P * jj : P * jj + P])
             else:
@@ -157,11 +174,11 @@ def tile_coattentionlayer_pa_t_kernel(tc, comp_feat, prot_feat, W_comp, b_comp, 
                 xq_of[n] = (codes, scales)
             nc.vector.quantize_mx(out=codes[:].bitcast(FP8X4), scales=scales[:], in_=xg_of[n][:])
 
-        def first_stage(g):
+        def first_stage(g, js=range(4)):
             n = GROUPS[g]
             kind, i, width = SOURCES[n]
             xc, xs = xq_of[n]
-            for j in range(4):
+            for j in js:
                 wc, ws = w_q[(0 if kind == "c" else 1, j)]
                 z = ps_z.tile([P, 512], F32, name="z", tag="z")
                 z_of[(g, j)] = z
@@ -188,13 +205,35 @@ def tile_coattentionlayer_pa_t_kernel(tc, comp_feat, prot_feat, W_comp, b_comp, 
                     scale=1.0,
                 )
 
-        def regroup(g):
+        def new_regrouped(g):
+            gr_new = gp.tile([P, 4 * SOURCES[GROUPS[g]][2]], BF16, name="gr", tag="gr", align_bytes=64)
+            gr_of[g] = gr_new
+
+        def gpsimd_tokens(g):
+            return GP_TOKENS if (SOURCES[GROUPS[g]][2] == 512 and GP_FIRST <= g <= GP_LAST) else 0
+
+        def regroup_vector(g):
             width = SOURCES[GROUPS[g]][2]
-            gr = gp.tile([P, 4 * width], BF16, name="gr", tag="gr", align_bytes=64)
-            gr_of[g] = gr
+            w0 = width - gpsimd_tokens(g)
+            th = th_of[g][:].rearrange("p (j n) -> p j n", j=4)
             nc.vector.tensor_copy(
-                out=gr[:].rearrange("p (c i j) -> p c j i", i=4, j=4),
-                in_=th_of[g][:].rearrange("p (j c i) -> p c j i", j=4, i=4),
+                out=gr_of[g][:, : 4 * w0].rearrange("p (c i j) -> p c j i", i=4, j=4),
+                in_=th[:, :, :w0].rearrange("p j (c i) -> p c j i", i=4),
+            )
+
+        def regroup_gpsimd(g):
+            width = SOURCES[GROUPS[g]][2]
+            w0 = width - gpsimd_tokens(g)
+            if w0 == width:
+                return
+            th = th_of[g][:].rearrange("p (j n) -> p j n", j=4)
+            nc.gpsimd.tensor_scalar(
+                out=gr_of[g][:, 4 * w0 :].rearrange("p (n j) -> p n j", j=4),
+                in0=th[:, :, w0:].rearrange("p j n -> p n j"),
+                scalar1=1.0,
+                scalar2=0.0,
+                op0=MULT,
+                op1=ADD,
             )
 
         def quantise_trans(g):
@@ -212,7 +251,10 @@ def tile_coattentionlayer_pa_t_kernel(tc, comp_feat, prot_feat, W_comp, b_comp, 
             p_codes, p_scales = tq_of[g]
             for un, (b, rs, c0, width, n0) in enumerate(units_of(g)):
                 c_codes, c_scales, off = comp_q[b]
-                o = ps_o.tile([P, 512], F32, name="o", tag="o")
+                if g >= WIDE_FROM and g % 2:
+                    o = ps_xt.tile([P, 512], F32, name="xt", tag="xt")
+                else:
+                    o = ps_o.tile([P, 512], F32, name="o", tag="o")
                 o_of[(g, un)] = o
                 for q, r in enumerate(rs):
                     m0 = off + P * r
@@ -234,22 +276,22 @@ def tile_coattentionlayer_pa_t_kernel(tc, comp_feat, prot_feat, W_comp, b_comp, 
             ot = out_tiles[b]
             o = o_of[(g, un)]
             if len(rs) == 1:
-                copy_out(engine, ot[:, LP * rs[0] + n0 : LP * rs[0] + n0 + width], o[:])
+                copy_out(engine, ot[:, LP * rs[0] + n0 : LP * rs[0] + n0 + width], o[:, :width])
             else:
                 copy_out(
                     engine,
                     ot[:].rearrange("p (r n) -> p r n", r=2)[:, :, n0 : n0 + width],
-                    o[:].rearrange("p (r n) -> p r n", r=2),
+                    o[:, : 2 * width].rearrange("p (r n) -> p r n", r=2),
                 )
 
         def stores(g):
             done = []
             for b, rs, c0, width, n0 in units_of(g):
-                if b == B - 1:
-                    if (b, n0, n0 + width) not in done:
-                        done.append((b, n0, n0 + width))
-                elif n0 + width == LP and (b, 0, LP) not in done:
-                    done.append((b, 0, LP))
+                if g < FINE_FROM:
+                    if n0 + width == LP and (b, 0, LP) not in done:
+                        done.append((b, 0, LP))
+                elif (b, n0, n0 + width) not in done:
+                    done.append((b, n0, n0 + width))
             for b, n0, n1 in done:
                 nc.sync.dma_start(
                     out=out[b].rearrange("(a r) n -> a r n", r=2)[:, :, n0:n1],
@@ -257,53 +299,88 @@ def tile_coattentionlayer_pa_t_kernel(tc, comp_feat, prot_feat, W_comp, b_comp, 
                 )
 
         def o_engine(g, un):
-            return "v" if (FIRST_VECTOR_O_GROUP <= g <= LAST_VECTOR_O_GROUP and un == 0) else "s"
+            return "v" if (g in EXTRA and un == 0) else "s"
 
-        for n, engine in ((0, "v"), (1, "s"), (2, "v"), (3, "s")):
+        for n in range(5):
             transposes(n)
-            copy_source(n, 0, engine)
-            quantise_source(n)
-        transposes(4)
-        copy_source(4, 0, "v")
-        copy_source(4, 1, "s")
+        copy_source(0, 0, "s")
+        copy_source(1, 0, "v")
+        quantise_source(0)
+        copy_source(1, 1, "s")
+        copy_source(2, 0, "s")
+        copy_source(3, 0, "v")
+        copy_source(4, 0, "s")
+        quantise_source(1)
+        quantise_source(2)
+        quantise_source(3)
+        quantise_source(4)
+        transposes(5)
+        copy_source(5, 0, "s")
+        copy_source(5, 1, "s")
         first_stage(0)
-        copied = [4]
-        next_source = 5
+        tanh(0)
+        quantise_source(5)
+        transposes(6)
+        first_stage(1)
+        copy_source(6, 0, "v")
+        copy_source(6, 1, "v")
+        tanh(1)
+        quantise_source(6)
+        transposes(7)
+        copy_source(7, 0, "v")
+        copy_source(7, 1, "s")
+        first_stage(2)
+        new_regrouped(0)
+        regroup_vector(0)
+        transposes(8)
+        copy_source(8, 0, "v")
+        copied = [7, 8]
+        next_source = 9
+        tanh(2)
+        copy_source(8, 1, "s")
 
-        for s in range(N_GROUPS + 3):
+
+        for s in range(2, N_GROUPS + AFF_LAG + 1):
             new = []
             target = GROUPS[min(N_GROUPS - 1, s + LEAD)] if s < N_GROUPS else len(SOURCES) - 1
             while next_source <= target and len(new) < 2:
                 new.append(next_source)
                 next_source += 1
-            g2 = s - 2
+            g2 = s - AFF_LAG
             n_units = len(units_of(g2)) if 0 <= g2 < N_GROUPS else 0
+            ends = s >= TAIL
+            for n in copied:
+                quantise_source(n)
+            copied = []
+            if s - 2 < min(N_GROUPS, TAIL - 1):
+                quantise_trans(s - 2)
             for n in new:
                 transposes(n)
             if n_units:
                 second_stage(g2)
-            if 0 <= s - 1 < N_GROUPS:
-                regroup(s - 1)
-            for n in copied:
-                quantise_source(n)
-            copied = []
             if s + 1 < N_GROUPS:
                 first_stage(s + 1)
-            if s < N_GROUPS:
+            if 2 < s < N_GROUPS:
                 tanh(s)
-            for un in range(n_units):
-                if o_engine(g2, un) == "s":
-                    affinity_out(g2, un, "s")
+            if s - 1 < N_GROUPS:
+                new_regrouped(s - 1)
+                regroup_gpsimd(s - 1)
             for engine in "vs":
                 for n in new:
                     for h in range(SOURCES[n][2] // 256):
                         if ("s" if (s <= LAST_SCALAR_B_STEP and h == 1) else "v") == engine:
                             copy_source(n, h, engine)
             copied = list(new)
-            if 0 <= s - 1 < N_GROUPS:
+            for un in range(n_units):
+                if o_engine(g2, un) == "s":
+                    affinity_out(g2, un, "s")
+            if ends and s - 1 < N_GROUPS:
+                regroup_vector(s - 1)
                 quantise_trans(s - 1)
             for un in range(n_units):
                 if o_engine(g2, un) == "v":
                     affinity_out(g2, un, "v")
+            if not ends and s - 1 < N_GROUPS:
+                regroup_vector(s - 1)
             if n_units:
                 stores(g2)

@@ -22,12 +22,12 @@ GPB = 1
 TAIL = 18
 FINE_FROM = 14
 AFF_LAG = 3
-EXTRA = (6,9,12,14,17)
-GP_TOKENS = 192
+EXTRA = (14,17)
+GP_TOKENS = 0
 GP_FIRST = 2
 GP_LAST = 14
 WARM_MATMULS = 3
-LAST_SCALAR_B_STEP = 7
+LAST_SCALAR_B_STEP = 8
 LAST_RAMP_SOURCE = 11
 
 SOURCES = (

@@ -17,18 +17,23 @@ B, LC, LP, D = 8, 256, 768, 512
 FLOPS = 2 * B * (LC + LP) * D * D + 2 * B * LC * LP * D
 
 LEAD = 3
+FS_EARLY = 1
+SB = ()
+VORDER = 2
+SECOND_FIRST = 1
+AFFBEFORE = 0
 WIDE_FROM = 13
-GPB = 1
+GPB = 3
 TAIL = 18
-FINE_FROM = 14
-AFF_LAG = 3
-EXTRA = (14,17)
+FINE_FROM = 11
+AFF_LAG = 2
+EXTRA = ()
 GP_TOKENS = 0
 GP_FIRST = 2
 GP_LAST = 14
-WARM_MATMULS = 3
+WARM_MATMULS = 2
 LAST_SCALAR_B_STEP = 8
-LAST_RAMP_SOURCE = 11
+LAST_RAMP_SOURCE = 14
 
 SOURCES = (
     [("w", (0, 0), 128), ("c", 0, 256), ("w", (0, 1), 128), ("w", (0, 2), 128), ("w", (0, 3), 128), ("c", 1, 256)]
@@ -50,7 +55,7 @@ def units_of(g):
     while t < t0 + width:
         b = t // LP
         end = min(t0 + width, (b + 1) * LP)
-        if end - t == 512 or g == N_GROUPS - 1:
+        if end - t == 512 or g >= N_GROUPS - 2:
             units.append((b, [0], t - t0, end - t, t - LP * b))
             units.append((b, [1], t - t0, end - t, t - LP * b))
         else:
@@ -283,6 +288,16 @@ def tile_coattentionlayer_pa_t_kernel(tc, comp_feat, prot_feat, W_comp, b_comp, 
                     ot[:].rearrange("p (r n) -> p r n", r=2)[:, :, n0 : n0 + width],
                     o[:, : 2 * width].rearrange("p (r n) -> p r n", r=2),
                 )
+            if g >= FINE_FROM:
+                unit_store(g, un)
+
+        def unit_store(g, un):
+            b, rs, c0, width, n0 = units_of(g)[un]
+            r0, r1 = rs[0], rs[-1] + 1
+            nc.sync.dma_start(
+                out=out[b].rearrange("(a r) n -> a r n", r=2)[:, r0:r1, n0 : n0 + width],
+                in_=out_tiles[b][:].rearrange("p (r n) -> p r n", r=2)[:, r0:r1, n0 : n0 + width],
+            )
 
         def stores(g):
             done = []
@@ -323,24 +338,25 @@ def tile_coattentionlayer_pa_t_kernel(tc, comp_feat, prot_feat, W_comp, b_comp, 
         transposes(6)
         first_stage(1)
         copy_source(6, 0, "v")
-        copy_source(6, 1, "v")
+        copy_source(6, 1, "s")
         tanh(1)
+        new_regrouped(0)
+        regroup_vector(0)
         quantise_source(6)
         transposes(7)
         copy_source(7, 0, "v")
         copy_source(7, 1, "s")
+        quantise_trans(0)
         first_stage(2)
-        new_regrouped(0)
-        regroup_vector(0)
         transposes(8)
+        quantise_source(7)
         copy_source(8, 0, "v")
-        copied = [7, 8]
+        copied = [8]
         next_source = 9
         tanh(2)
         copy_source(8, 1, "s")
 
-
-        for s in range(2, N_GROUPS + AFF_LAG + 1):
+        for s in range(2, 15):
             new = []
             target = GROUPS[min(N_GROUPS - 1, s + LEAD)] if s < N_GROUPS else len(SOURCES) - 1
             while next_source <= target and len(new) < 2:
@@ -349,38 +365,104 @@ def tile_coattentionlayer_pa_t_kernel(tc, comp_feat, prot_feat, W_comp, b_comp, 
             g2 = s - AFF_LAG
             n_units = len(units_of(g2)) if 0 <= g2 < N_GROUPS else 0
             ends = s >= TAIL
-            for n in copied:
-                quantise_source(n)
-            copied = []
-            if s - 2 < min(N_GROUPS, TAIL - 1):
-                quantise_trans(s - 2)
-            for n in new:
-                transposes(n)
-            if n_units:
-                second_stage(g2)
-            if s + 1 < N_GROUPS:
+            if s > FS_EARLY:
+                for n in new:
+                    transposes(n)
+            if VORDER == 0:
+                for n in copied:
+                    quantise_source(n)
+                if 0 <= s - 2 < min(N_GROUPS, TAIL - 1):
+                    quantise_trans(s - 2)
+            else:
+                if 1 <= s - 1 < N_GROUPS:
+                    new_regrouped(s - 1)
+                    regroup_vector(s - 1)
+                if ends and s - 1 < N_GROUPS:
+                    quantise_trans(s - 1)
+                if VORDER == 1:
+                    for n in copied:
+                        quantise_source(n)
+            if s <= FS_EARLY and s + 1 < N_GROUPS:
                 first_stage(s + 1)
+            if s <= FS_EARLY:
+                for n in new:
+                    transposes(n)
+            if n_units and SECOND_FIRST:
+                second_stage(g2)
+            if s > FS_EARLY and s + 1 < N_GROUPS:
+                first_stage(s + 1)
+            if n_units and not SECOND_FIRST:
+                second_stage(g2)
             if 2 < s < N_GROUPS:
                 tanh(s)
-            if s - 1 < N_GROUPS:
-                new_regrouped(s - 1)
-                regroup_gpsimd(s - 1)
+            if AFFBEFORE:
+                for un in range(n_units):
+                    if o_engine(g2, un) == "s":
+                        affinity_out(g2, un, "s")
             for engine in "vs":
                 for n in new:
                     for h in range(SOURCES[n][2] // 256):
-                        if ("s" if (s <= LAST_SCALAR_B_STEP and h == 1) else "v") == engine:
+                        if ("s" if ((s <= LAST_SCALAR_B_STEP or s in SB) and h == 1) else "v") == engine:
                             copy_source(n, h, engine)
+            quants = list(copied)
             copied = list(new)
-            for un in range(n_units):
-                if o_engine(g2, un) == "s":
-                    affinity_out(g2, un, "s")
-            if ends and s - 1 < N_GROUPS:
-                regroup_vector(s - 1)
-                quantise_trans(s - 1)
-            for un in range(n_units):
-                if o_engine(g2, un) == "v":
-                    affinity_out(g2, un, "v")
-            if not ends and s - 1 < N_GROUPS:
-                regroup_vector(s - 1)
-            if n_units:
+            if not AFFBEFORE:
+                for un in range(n_units):
+                    if o_engine(g2, un) == "s":
+                        affinity_out(g2, un, "s")
+            if VORDER == 0:
+                if ends and s - 1 < N_GROUPS:
+                    new_regrouped(s - 1)
+                    regroup_vector(s - 1)
+                    quantise_trans(s - 1)
+                for un in range(n_units):
+                    if o_engine(g2, un) == "v":
+                        affinity_out(g2, un, "v")
+                if not ends and s - 1 < N_GROUPS:
+                    new_regrouped(s - 1)
+                    regroup_vector(s - 1)
+            else:
+                if not ends and 1 <= s - 1 < N_GROUPS:
+                    quantise_trans(s - 1)
+                if VORDER == 2:
+                    for n in quants:
+                        quantise_source(n)
+                for un in range(n_units):
+                    if o_engine(g2, un) == "v":
+                        affinity_out(g2, un, "v")
+            if n_units and g2 < FINE_FROM:
                 stores(g2)
+
+        second_stage(13)
+        first_stage(16)
+        new_regrouped(14)
+        regroup_vector(14)
+        quantise_source(copied[0])
+        quantise_trans(14)
+        tanh(15)
+        affinity_out(13, 0, "v")
+        affinity_out(13, 1, "s")
+        tanh(16)
+        second_stage(14)
+        first_stage(17)
+        new_regrouped(15)
+        regroup_vector(15)
+        affinity_out(14, 0, "v")
+        quantise_trans(15)
+        new_regrouped(16)
+        regroup_vector(16)
+        tanh(17)
+        affinity_out(14, 1, "s")
+        second_stage(15)
+        new_regrouped(17)
+        regroup_vector(17)
+        quantise_trans(16)
+        quantise_trans(17)
+        affinity_out(15, 0, "s")
+        affinity_out(15, 1, "s")
+        second_stage(16)
+        second_stage(17)
+        affinity_out(16, 0, "v")
+        affinity_out(16, 1, "s")
+        affinity_out(17, 0, "v")
+        affinity_out(17, 1, "s")

@@ -27,16 +27,16 @@ GPB = 3
 TAIL = 18
 FINE_FROM = 11
 AFF_LAG = 2
-EXTRA = ()
+EXTRA = (8, 12)
 GP_TOKENS = 0
 GP_FIRST = 2
 GP_LAST = 14
 WARM_MATMULS = 2
-LAST_SCALAR_B_STEP = 8
-LAST_RAMP_SOURCE = 14
+LAST_SCALAR_B_STEP = 7
+LAST_RAMP_SOURCE = 12
 
 SOURCES = (
-    [("w", (0, 0), 128), ("c", 0, 256), ("w", (0, 1), 128), ("w", (0, 2), 128), ("w", (0, 3), 128), ("c", 1, 256)]
+    [("w", (0, 0), 256), ("c", 0, 256), ("w", (0, 1), 256), ("c", 1, 256)]
     + [("c", b, 512) for b in (2, 4, 6)]
     + [("w", (1, None), 512)]
     + [("p", 512 * i, 512) for i in range(11)]
@@ -83,11 +83,11 @@ def tile_coattentionlayer_pa_t_kernel(tc, comp_feat, prot_feat, W_comp, b_comp, 
 
         prot_flat = prot_feat.flatten_outer_dims()
 
-        bias = []
+        bias_bf = []
         for w, b_ap in enumerate((b_comp, b_prot)):
-            bt = const.tile([P, 4], BF16, name="bias%d" % w)
+            bt = const.tile([P, 4], BF16, name="bias_bf%d" % w)
             nc.scalar.dma_start(out=bt[:], in_=b_ap.rearrange("(p j) -> p j", j=4))
-            bias.append(bt)
+            bias_bf.append(bt)
 
         warm = const.tile([P, 1], F32, name="warm")
         nc.vector.memset(warm[:], 0.0)
@@ -109,7 +109,7 @@ def tile_coattentionlayer_pa_t_kernel(tc, comp_feat, prot_feat, W_comp, b_comp, 
             if kind == "w":
                 w_ap = (W_comp, W_prot)[i[0]].rearrange("(p j) k -> p j k", j=4)
                 if i[1] is not None:
-                    w_ap = w_ap[:, i[1] : i[1] + 1, :]
+                    w_ap = w_ap[:, 2 * i[1] : 2 * i[1] + 2, :]
                 nc.sync.dma_start(out=x[:].rearrange("p (j k) -> p j k", k=D), in_=w_ap)
             elif kind == "c":
                 src = comp_feat[i : i + width // LC].rearrange("b (p r) k -> p b (r k)", r=2)
@@ -118,6 +118,14 @@ def tile_coattentionlayer_pa_t_kernel(tc, comp_feat, prot_feat, W_comp, b_comp, 
                 src = prot_flat[i : i + width, :].rearrange("(t p) k -> p t k", p=P)
                 nc.sync.dma_start(out=x[:].rearrange("p (t k) -> p t k", k=D), in_=src)
             raw.append(x)
+
+        bias = []
+
+        def cast_biases():
+            for w in range(2):
+                bt = const.tile([P, 4], F32, name="bias%d" % w)
+                nc.vector.tensor_copy(out=bt[:], in_=bias_bf[w][:])
+                bias.append(bt)
 
         def copy_out(engine, dst, src):
             if engine == "v":
@@ -130,7 +138,7 @@ def tile_coattentionlayer_pa_t_kernel(tc, comp_feat, prot_feat, W_comp, b_comp, 
         ramp_banks = []
 
         def tiles_of(n):
-            return 1 if SOURCES[n][2] <= 256 and n < 6 else 2
+            return 1 if SOURCES[n][2] <= 256 and n < 4 else 2
 
         def banks_of(n):
             return range(SOURCES[n][2] // (P * tiles_of(n)))
@@ -170,7 +178,7 @@ def tile_coattentionlayer_pa_t_kernel(tc, comp_feat, prot_feat, W_comp, b_comp, 
             if kind == "w":
                 codes = const.tile([P, width], U32, name="wc%d" % n, align_bytes=64)
                 scales = const.tile([P, width], U8, name="ws%d" % n, align_bytes=64)
-                first_j = 0 if i[1] is None else i[1]
+                first_j = 0 if i[1] is None else 2 * i[1]
                 for jj in range(width // P):
                     w_q[(i[0], first_j + jj)] = (codes[:, P * jj : P * jj + P], scales[:, P * jj : P * jj + P])
             else:
@@ -316,45 +324,44 @@ def tile_coattentionlayer_pa_t_kernel(tc, comp_feat, prot_feat, W_comp, b_comp, 
         def o_engine(g, un):
             return "v" if (g in EXTRA and un == 0) else "s"
 
-        for n in range(5):
+        for n in range(4):
             transposes(n)
         copy_source(0, 0, "s")
-        copy_source(1, 0, "v")
+        copy_source(0, 1, "v")
+        copy_source(1, 0, "s")
+        copy_source(1, 1, "v")
         quantise_source(0)
-        copy_source(1, 1, "s")
         copy_source(2, 0, "s")
-        copy_source(3, 0, "v")
-        copy_source(4, 0, "s")
+        copy_source(2, 1, "v")
         quantise_source(1)
+        first_stage(0, [0, 1])
         quantise_source(2)
-        quantise_source(3)
-        quantise_source(4)
-        transposes(5)
-        copy_source(5, 0, "s")
-        copy_source(5, 1, "s")
-        first_stage(0)
+        first_stage(0, [2, 3])
+        copy_source(3, 0, "s")
+        cast_biases()
+        copy_source(3, 1, "v")
         tanh(0)
-        quantise_source(5)
-        transposes(6)
+        quantise_source(3)
+        transposes(4)
         first_stage(1)
-        copy_source(6, 0, "v")
-        copy_source(6, 1, "s")
+        copy_source(4, 0, "v")
+        copy_source(4, 1, "s")
         tanh(1)
         new_regrouped(0)
         regroup_vector(0)
-        quantise_source(6)
-        transposes(7)
-        copy_source(7, 0, "v")
-        copy_source(7, 1, "s")
+        quantise_source(4)
+        transposes(5)
+        copy_source(5, 0, "v")
+        copy_source(5, 1, "s")
         quantise_trans(0)
         first_stage(2)
-        transposes(8)
-        quantise_source(7)
-        copy_source(8, 0, "v")
-        copied = [8]
-        next_source = 9
+        transposes(6)
+        quantise_source(5)
+        copy_source(6, 0, "v")
+        copied = [6]
+        next_source = 7
         tanh(2)
-        copy_source(8, 1, "s")
+        copy_source(6, 1, "s")
 
         for s in range(2, 15):
             new = []

@@ -27,12 +27,12 @@ GPB = 3
 TAIL = 18
 FINE_FROM = 11
 AFF_LAG = 2
-EXTRA = (8, 12)
+EXTRA = ()
 GP_TOKENS = 0
 GP_FIRST = 2
 GP_LAST = 14
 WARM_MATMULS = 2
-LAST_SCALAR_B_STEP = 7
+LAST_SCALAR_B_STEP = 8
 LAST_RAMP_SOURCE = 12
 
 SOURCES = (

@@ -8,8 +8,6 @@ BF16 = mybir.dt.bfloat16
 U32 = mybir.dt.uint32
 U8 = mybir.dt.uint8
 FP8X4 = mybir.dt.float8_e4m3fn_x4
-MULT = mybir.AluOpType.mult
-ADD = mybir.AluOpType.add
 TANH = mybir.ActivationFunctionType.Tanh
 
 P = 128
@@ -17,23 +15,12 @@ B, LC, LP, D = 8, 256, 768, 512
 FLOPS = 2 * B * (LC + LP) * D * D + 2 * B * LC * LP * D
 
 LEAD = 3
-FS_EARLY = 1
-SB = ()
-VORDER = 2
-SECOND_FIRST = 1
-AFFBEFORE = 0
-WIDE_FROM = 13
-GPB = 3
-TAIL = 18
-FINE_FROM = 11
-AFF_LAG = 2
-EXTRA = ()
-GP_TOKENS = 0
-GP_FIRST = 2
-GP_LAST = 14
 WARM_MATMULS = 2
-LAST_SCALAR_B_STEP = 8
+LAST_SCALAR_B_STEP = 7
 LAST_RAMP_SOURCE = 12
+EXTRA = ()
+LAST_FULL_STORE_GROUP = 13
+LAST_LOOP_STEP = 14
 
 SOURCES = (
     [("w", (0, 0), 256), ("c", 0, 256), ("w", (0, 1), 256), ("c", 1, 256)]
@@ -70,10 +57,10 @@ def tile_coattentionlayer_pa_t_kernel(tc, comp_feat, prot_feat, W_comp, b_comp, 
         ctx.enter_context(tc.manual_schedule())
         const = ctx.enter_context(tc.tile_pool(name="const", bufs=1))
         xin = ctx.enter_context(tc.tile_pool(name="xin", bufs=1))
-        xgp = ctx.enter_context(tc.tile_pool(name="xgp", bufs=6))
-        xqp = ctx.enter_context(tc.tile_pool(name="xqp", bufs=6))
+        xgp = ctx.enter_context(tc.tile_pool(name="xgp", bufs=3))
+        xqp = ctx.enter_context(tc.tile_pool(name="xqp", bufs=4))
         tp = ctx.enter_context(tc.tile_pool(name="tp", bufs=3))
-        gp = ctx.enter_context(tc.tile_pool(name="gp", bufs=GPB))
+        gp = ctx.enter_context(tc.tile_pool(name="gp", bufs=3))
         cq = ctx.enter_context(tc.tile_pool(name="cq", bufs=5))
         pq = ctx.enter_context(tc.tile_pool(name="pq", bufs=5))
         op = ctx.enter_context(tc.tile_pool(name="op", bufs=4))
@@ -133,20 +120,23 @@ def tile_coattentionlayer_pa_t_kernel(tc, comp_feat, prot_feat, W_comp, b_comp, 
             else:
                 nc.scalar.copy(out=dst, in_=src)
 
-        xt_of, xg_of, xq_of, w_q = {}, {}, {}, {}
-        z_of, th_of, gr_of, tq_of, comp_q, o_of, out_tiles = {}, {}, {}, {}, {}, {}, {}
+        xt_of, grouped, regrouped = {}, {}, {}
+        x_q, t_q, w_q, comp_q = {}, {}, {}, {}
+        z_of, th_of, o_of, out_tiles = {}, {}, {}, {}
         ramp_banks = []
 
         def tiles_of(n):
-            return 1 if SOURCES[n][2] <= 256 and n < 4 else 2
+            return 2
 
         def banks_of(n):
             return range(SOURCES[n][2] // (P * tiles_of(n)))
 
-        def transposes(n):
+        def transposes(n, banks=None):
             xf = raw[n][:].bitcast(F32)
             for h in banks_of(n):
-                if n <= LAST_RAMP_SOURCE and len(ramp_banks) % 2 == 1:
+                if banks is not None and banks[h] == "z":
+                    xt = ps_z.tile([P, 512], F32, name="z", tag="z")
+                elif (banks is None and n <= LAST_RAMP_SOURCE and len(ramp_banks) % 2 == 1) or (banks is not None and banks[h] == "o"):
                     xt = ps_o.tile([P, 512], F32, name="o", tag="o")
                 else:
                     xt = ps_xt.tile([P, 512], F32, name="xt", tag="xt")
@@ -161,11 +151,14 @@ def tile_coattentionlayer_pa_t_kernel(tc, comp_feat, prot_feat, W_comp, b_comp, 
                             ident[:],
                         )
 
+        def place_of(n):
+            if n not in grouped:
+                xg = xgp.tile([P, 4 * SOURCES[n][2]], BF16, name="xg", tag="xg", align_bytes=64)
+                grouped[n] = xg[:]
+            return grouped[n]
+
         def copy_source(n, h, engine):
-            if n not in xg_of:
-                xg_new = xgp.tile([P, 4 * SOURCES[n][2]], BF16, name="xg", tag="xg", align_bytes=64)
-                xg_of[n] = xg_new
-            xgf = xg_of[n][:].bitcast(F32)
+            xgf = place_of(n).bitcast(F32)
             nt = tiles_of(n)
             copy_out(
                 engine,
@@ -184,13 +177,28 @@ def tile_coattentionlayer_pa_t_kernel(tc, comp_feat, prot_feat, W_comp, b_comp, 
             else:
                 codes = xqp.tile([P, width], U32, name="xc", tag="xc", align_bytes=64)
                 scales = xqp.tile([P, width], U8, name="xs", tag="xs", align_bytes=64)
-                xq_of[n] = (codes, scales)
-            nc.vector.quantize_mx(out=codes[:].bitcast(FP8X4), scales=scales[:], in_=xg_of[n][:])
+                x_q[n] = (codes[:], scales[:])
+            nc.vector.quantize_mx(out=codes[:].bitcast(FP8X4), scales=scales[:], in_=grouped[n])
+
+        def keep_trans(g, codes, scales):
+            kind, i, width = SOURCES[GROUPS[g]]
+            t_q[g] = (codes, scales)
+            if kind == "c":
+                for bb in range(width // LC):
+                    comp_q[i + bb] = (codes, scales, LC * bb)
+
+        def quantise_trans(g):
+            kind, i, width = SOURCES[GROUPS[g]]
+            pool = cq if kind == "c" else pq
+            tcd = pool.tile([P, width], U32, name="tcd", tag="tcd", align_bytes=64)
+            tsc = pool.tile([P, width], U8, name="tsc", tag="tsc", align_bytes=64)
+            keep_trans(g, tcd[:], tsc[:])
+            nc.vector.quantize_mx(out=tcd[:].bitcast(FP8X4), scales=tsc[:], in_=regrouped[g])
 
         def first_stage(g, js=range(4)):
             n = GROUPS[g]
             kind, i, width = SOURCES[n]
-            xc, xs = xq_of[n]
+            xc, xs = x_q[n]
             for j in js:
                 wc, ws = w_q[(0 if kind == "c" else 1, j)]
                 z = ps_z.tile([P, 512], F32, name="z", tag="z")
@@ -199,8 +207,8 @@ def tile_coattentionlayer_pa_t_kernel(tc, comp_feat, prot_feat, W_comp, b_comp, 
                     out=z[:, :width],
                     lhsT=wc.bitcast(FP8X4),
                     lhsT_scale=ws,
-                    rhs=xc[:].bitcast(FP8X4),
-                    rhs_scale=xs[:],
+                    rhs=xc.bitcast(FP8X4),
+                    rhs_scale=xs,
                     start=True,
                     stop=True,
                 )
@@ -218,53 +226,20 @@ def tile_coattentionlayer_pa_t_kernel(tc, comp_feat, prot_feat, W_comp, b_comp, 
                     scale=1.0,
                 )
 
-        def new_regrouped(g):
-            gr_new = gp.tile([P, 4 * SOURCES[GROUPS[g]][2]], BF16, name="gr", tag="gr", align_bytes=64)
-            gr_of[g] = gr_new
-
-        def gpsimd_tokens(g):
-            return GP_TOKENS if (SOURCES[GROUPS[g]][2] == 512 and GP_FIRST <= g <= GP_LAST) else 0
-
-        def regroup_vector(g):
+        def regroup(g):
             width = SOURCES[GROUPS[g]][2]
-            w0 = width - gpsimd_tokens(g)
-            th = th_of[g][:].rearrange("p (j n) -> p j n", j=4)
+            gr = gp.tile([P, 4 * width], BF16, name="gr", tag="gr", align_bytes=64)
+            regrouped[g] = gr[:]
             nc.vector.tensor_copy(
-                out=gr_of[g][:, : 4 * w0].rearrange("p (c i j) -> p c j i", i=4, j=4),
-                in_=th[:, :, :w0].rearrange("p j (c i) -> p c j i", i=4),
+                out=regrouped[g].rearrange("p (c i j) -> p c j i", i=4, j=4),
+                in_=th_of[g][:].rearrange("p (j c i) -> p c j i", j=4, i=4),
             )
 
-        def regroup_gpsimd(g):
-            width = SOURCES[GROUPS[g]][2]
-            w0 = width - gpsimd_tokens(g)
-            if w0 == width:
-                return
-            th = th_of[g][:].rearrange("p (j n) -> p j n", j=4)
-            nc.gpsimd.tensor_scalar(
-                out=gr_of[g][:, 4 * w0 :].rearrange("p (n j) -> p n j", j=4),
-                in0=th[:, :, w0:].rearrange("p j n -> p n j"),
-                scalar1=1.0,
-                scalar2=0.0,
-                op0=MULT,
-                op1=ADD,
-            )
-
-        def quantise_trans(g):
-            kind, i, width = SOURCES[GROUPS[g]]
-            pool = cq if kind == "c" else pq
-            tcd = pool.tile([P, width], U32, name="tcd", tag="tcd", align_bytes=64)
-            tsc = pool.tile([P, width], U8, name="tsc", tag="tsc", align_bytes=64)
-            tq_of[g] = (tcd, tsc)
-            if kind == "c":
-                for bb in range(width // LC):
-                    comp_q[i + bb] = (tcd, tsc, LC * bb)
-            nc.vector.quantize_mx(out=tcd[:].bitcast(FP8X4), scales=tsc[:], in_=gr_of[g][:])
-
-        def second_stage(g):
-            p_codes, p_scales = tq_of[g]
+        def second_stage(g, wide=False):
+            p_codes, p_scales = t_q[g]
             for un, (b, rs, c0, width, n0) in enumerate(units_of(g)):
                 c_codes, c_scales, off = comp_q[b]
-                if g >= WIDE_FROM and g % 2:
+                if wide:
                     o = ps_xt.tile([P, 512], F32, name="xt", tag="xt")
                 else:
                     o = ps_o.tile([P, 512], F32, name="o", tag="o")
@@ -281,6 +256,12 @@ def tile_coattentionlayer_pa_t_kernel(tc, comp_feat, prot_feat, W_comp, b_comp, 
                         stop=True,
                     )
 
+        def store(b, r0, r1, n0, n1):
+            nc.sync.dma_start(
+                out=out[b].rearrange("(a r) n -> a r n", r=2)[:, r0:r1, n0:n1],
+                in_=out_tiles[b][:].rearrange("p (r n) -> p r n", r=2)[:, r0:r1, n0:n1],
+            )
+
         def affinity_out(g, un, engine):
             b, rs, c0, width, n0 = units_of(g)[un]
             if b not in out_tiles:
@@ -296,179 +277,111 @@ def tile_coattentionlayer_pa_t_kernel(tc, comp_feat, prot_feat, W_comp, b_comp, 
                     ot[:].rearrange("p (r n) -> p r n", r=2)[:, :, n0 : n0 + width],
                     o[:, : 2 * width].rearrange("p (r n) -> p r n", r=2),
                 )
-            if g >= FINE_FROM:
-                unit_store(g, un)
+            if g > LAST_FULL_STORE_GROUP:
+                store(b, rs[0], rs[-1] + 1, n0, n0 + width)
 
-        def unit_store(g, un):
-            b, rs, c0, width, n0 = units_of(g)[un]
-            r0, r1 = rs[0], rs[-1] + 1
-            nc.sync.dma_start(
-                out=out[b].rearrange("(a r) n -> a r n", r=2)[:, r0:r1, n0 : n0 + width],
-                in_=out_tiles[b][:].rearrange("p (r n) -> p r n", r=2)[:, r0:r1, n0 : n0 + width],
-            )
+        def full_stores(g):
+            for b in range(B):
+                if g <= LAST_FULL_STORE_GROUP and any(u[0] == b and u[4] + u[3] == LP for u in units_of(g)):
+                    store(b, 0, 2, 0, LP)
 
-        def stores(g):
-            done = []
-            for b, rs, c0, width, n0 in units_of(g):
-                if g < FINE_FROM:
-                    if n0 + width == LP and (b, 0, LP) not in done:
-                        done.append((b, 0, LP))
-                elif (b, n0, n0 + width) not in done:
-                    done.append((b, n0, n0 + width))
-            for b, n0, n1 in done:
-                nc.sync.dma_start(
-                    out=out[b].rearrange("(a r) n -> a r n", r=2)[:, :, n0:n1],
-                    in_=out_tiles[b][:].rearrange("p (r n) -> p r n", r=2)[:, :, n0:n1],
-                )
-
-        def o_engine(g, un):
-            return "v" if (g in EXTRA and un == 0) else "s"
-
-        for n in range(4):
-            transposes(n)
-        copy_source(0, 0, "s")
-        copy_source(0, 1, "v")
+        transposes(0, "x")
+        transposes(1, "o")
+        transposes(2, "z")
+        transposes(3, "z")
+        transposes(4, "xo")
+        copy_source(0, 0, "v")
         copy_source(1, 0, "s")
-        copy_source(1, 1, "v")
         quantise_source(0)
-        copy_source(2, 0, "s")
-        copy_source(2, 1, "v")
+        copy_source(2, 0, "v")
         quantise_source(1)
-        first_stage(0, [0, 1])
-        quantise_source(2)
-        first_stage(0, [2, 3])
         copy_source(3, 0, "s")
+        quantise_source(2)
+        first_stage(0)
         cast_biases()
-        copy_source(3, 1, "v")
-        tanh(0)
         quantise_source(3)
-        transposes(4)
+        copy_source(4, 0, "s")
+        copy_source(4, 1, "v")
+        tanh(0)
+        transposes(5, "xo")
         first_stage(1)
-        copy_source(4, 0, "v")
-        copy_source(4, 1, "s")
-        tanh(1)
-        new_regrouped(0)
-        regroup_vector(0)
         quantise_source(4)
-        transposes(5)
         copy_source(5, 0, "v")
         copy_source(5, 1, "s")
-        quantise_trans(0)
-        first_stage(2)
-        transposes(6)
+        tanh(1)
+        regroup(0)
         quantise_source(5)
+        transposes(6, "xo")
+        first_stage(2)
+        quantise_trans(0)
         copy_source(6, 0, "v")
-        copied = [6]
-        next_source = 7
-        tanh(2)
         copy_source(6, 1, "s")
+        tanh(2)
+        regroup(1)
+        quantise_source(6)
+        copied = []
+        next_source = 7
 
-        for s in range(2, 15):
+        for s in range(2, LAST_LOOP_STEP + 1):
             new = []
-            target = GROUPS[min(N_GROUPS - 1, s + LEAD)] if s < N_GROUPS else len(SOURCES) - 1
+            target = GROUPS[min(N_GROUPS - 1, s + LEAD)]
             while next_source <= target and len(new) < 2:
                 new.append(next_source)
                 next_source += 1
-            g2 = s - AFF_LAG
-            n_units = len(units_of(g2)) if 0 <= g2 < N_GROUPS else 0
-            ends = s >= TAIL
-            if s > FS_EARLY:
-                for n in new:
-                    transposes(n)
-            if VORDER == 0:
-                for n in copied:
-                    quantise_source(n)
-                if 0 <= s - 2 < min(N_GROUPS, TAIL - 1):
-                    quantise_trans(s - 2)
-            else:
-                if 1 <= s - 1 < N_GROUPS:
-                    new_regrouped(s - 1)
-                    regroup_vector(s - 1)
-                if ends and s - 1 < N_GROUPS:
-                    quantise_trans(s - 1)
-                if VORDER == 1:
-                    for n in copied:
-                        quantise_source(n)
-            if s <= FS_EARLY and s + 1 < N_GROUPS:
-                first_stage(s + 1)
-            if s <= FS_EARLY:
-                for n in new:
-                    transposes(n)
-            if n_units and SECOND_FIRST:
+            g2 = s - 2
+            n_units = len(units_of(g2))
+            for n in new:
+                transposes(n)
+            if s > 2:
+                regroup(s - 1)
+            if n_units:
                 second_stage(g2)
-            if s > FS_EARLY and s + 1 < N_GROUPS:
-                first_stage(s + 1)
-            if n_units and not SECOND_FIRST:
-                second_stage(g2)
-            if 2 < s < N_GROUPS:
+            first_stage(s + 1)
+            if s > 2:
                 tanh(s)
-            if AFFBEFORE:
-                for un in range(n_units):
-                    if o_engine(g2, un) == "s":
-                        affinity_out(g2, un, "s")
             for engine in "vs":
                 for n in new:
-                    for h in range(SOURCES[n][2] // 256):
-                        if ("s" if ((s <= LAST_SCALAR_B_STEP or s in SB) and h == 1) else "v") == engine:
+                    for h in banks_of(n):
+                        if ("s" if (s <= LAST_SCALAR_B_STEP and h == 1) else "v") == engine:
                             copy_source(n, h, engine)
-            quants = list(copied)
+            for un in range(n_units):
+                if (g2, un) != (12, 0):
+                    affinity_out(g2, un, "v" if (g2 in EXTRA and un == 0) else "s")
+            if g2 != 12:
+                full_stores(g2)
+            quantise_trans(s - 1)
+            for n in copied:
+                quantise_source(n)
             copied = list(new)
-            if not AFFBEFORE:
-                for un in range(n_units):
-                    if o_engine(g2, un) == "s":
-                        affinity_out(g2, un, "s")
-            if VORDER == 0:
-                if ends and s - 1 < N_GROUPS:
-                    new_regrouped(s - 1)
-                    regroup_vector(s - 1)
-                    quantise_trans(s - 1)
-                for un in range(n_units):
-                    if o_engine(g2, un) == "v":
-                        affinity_out(g2, un, "v")
-                if not ends and s - 1 < N_GROUPS:
-                    new_regrouped(s - 1)
-                    regroup_vector(s - 1)
-            else:
-                if not ends and 1 <= s - 1 < N_GROUPS:
-                    quantise_trans(s - 1)
-                if VORDER == 2:
-                    for n in quants:
-                        quantise_source(n)
-                for un in range(n_units):
-                    if o_engine(g2, un) == "v":
-                        affinity_out(g2, un, "v")
-            if n_units and g2 < FINE_FROM:
-                stores(g2)
 
-        second_stage(13)
+        affinity_out(12, 0, "v")
+        second_stage(13, True)
         first_stage(16)
-        new_regrouped(14)
-        regroup_vector(14)
+        regroup(14)
         quantise_source(copied[0])
         quantise_trans(14)
+        full_stores(12)
         tanh(15)
         affinity_out(13, 0, "v")
         affinity_out(13, 1, "s")
+        full_stores(13)
         tanh(16)
         second_stage(14)
         first_stage(17)
-        new_regrouped(15)
-        regroup_vector(15)
-        affinity_out(14, 0, "v")
-        quantise_trans(15)
-        new_regrouped(16)
-        regroup_vector(16)
         tanh(17)
+        regroup(15)
+        quantise_trans(15)
+        regroup(16)
+        second_stage(15, True)
+        regroup(17)
+        affinity_out(14, 0, "s")
         affinity_out(14, 1, "s")
-        second_stage(15)
-        new_regrouped(17)
-        regroup_vector(17)
         quantise_trans(16)
         quantise_trans(17)
         affinity_out(15, 0, "s")
         affinity_out(15, 1, "s")
         second_stage(16)
-        second_stage(17)
+        second_stage(17, True)
         affinity_out(16, 0, "v")
         affinity_out(16, 1, "s")
         affinity_out(17, 0, "v")

@@ -231,8 +231,8 @@ def tile_coattentionlayer_pa_t_kernel(tc, comp_feat, prot_feat, W_comp, b_comp, 
             gr = gp.tile([P, 4 * width], BF16, name="gr", tag="gr", align_bytes=64)
             regrouped[g] = gr[:]
             nc.vector.tensor_copy(
-                out=regrouped[g].rearrange("p (c i j) -> p c j i", i=4, j=4),
-                in_=th_of[g][:].rearrange("p (j c i) -> p c j i", j=4, i=4),
+                out=regrouped[g].rearrange("p (c i j) -> p c j i", i=2, j=4),
+                in_=th_of[g][:].rearrange("p (j c i) -> p c j i", j=4, i=2),
             )
 
         def second_stage(g, wide=False):

from contextlib import ExitStack

import concourse.mybir as mybir
from concourse.masks import make_identity

F32 = mybir.dt.float32
BF16 = mybir.dt.bfloat16
U32 = mybir.dt.uint32
U8 = mybir.dt.uint8
FP8X4 = mybir.dt.float8_e4m3fn_x4
TANH = mybir.ActivationFunctionType.Tanh

P = 128
B, LC, LP, D = 8, 256, 768, 512
FLOPS = 2 * B * (LC + LP) * D * D + 2 * B * LC * LP * D

LEAD = 3
WARM_MATMULS = 2
LAST_SCALAR_B_STEP = 7
LAST_RAMP_SOURCE = 12
EXTRA = ()
LAST_FULL_STORE_GROUP = 13
LAST_LOOP_STEP = 14

SOURCES = (
    [("w", (0, 0), 256), ("c", 0, 256), ("w", (0, 1), 256), ("c", 1, 256)]
    + [("c", b, 512) for b in (2, 4, 6)]
    + [("w", (1, None), 512)]
    + [("p", 512 * i, 512) for i in range(11)]
    + [("p", 5632, 256), ("p", 5888, 256)]
)
GROUPS = [n for n in range(len(SOURCES)) if SOURCES[n][0] != "w"]
N_GROUPS = len(GROUPS)


def units_of(g):
    kind, t0, width = SOURCES[GROUPS[g]]
    if kind != "p":
        return []
    units = []
    t = t0
    while t < t0 + width:
        b = t // LP
        end = min(t0 + width, (b + 1) * LP)
        if end - t == 512 or g >= N_GROUPS - 2:
            units.append((b, [0], t - t0, end - t, t - LP * b))
            units.append((b, [1], t - t0, end - t, t - LP * b))
        else:
            units.append((b, [0, 1], t - t0, end - t, t - LP * b))
        t = end
    return units


def tile_coattentionlayer_pa_t_kernel(tc, comp_feat, prot_feat, W_comp, b_comp, W_prot, b_prot, out):
    nc = tc.nc
    with ExitStack() as ctx:
        ctx.enter_context(tc.manual_schedule())
        const = ctx.enter_context(tc.tile_pool(name="const", bufs=1))
        xin = ctx.enter_context(tc.tile_pool(name="xin", bufs=1))
        xgp = ctx.enter_context(tc.tile_pool(name="xgp", bufs=3))
        xqp = ctx.enter_context(tc.tile_pool(name="xqp", bufs=4))
        tp = ctx.enter_context(tc.tile_pool(name="tp", bufs=3))
        gp = ctx.enter_context(tc.tile_pool(name="gp", bufs=3))
        cq = ctx.enter_context(tc.tile_pool(name="cq", bufs=5))
        pq = ctx.enter_context(tc.tile_pool(name="pq", bufs=5))
        op = ctx.enter_context(tc.tile_pool(name="op", bufs=4))
        ps_xt = ctx.enter_context(tc.psum_pool(name="ps_xt", bufs=2))
        ps_z = ctx.enter_context(tc.psum_pool(name="ps_z", bufs=4))
        ps_o = ctx.enter_context(tc.psum_pool(name="ps_o", bufs=2))

        prot_flat = prot_feat.flatten_outer_dims()

        bias_bf = []
        for w, b_ap in enumerate((b_comp, b_prot)):
            bt = const.tile([P, 4], BF16, name="bias_bf%d" % w)
            nc.scalar.dma_start(out=bt[:], in_=b_ap.rearrange("(p j) -> p j", j=4))
            bias_bf.append(bt)

        warm = const.tile([P, 1], F32, name="warm")
        nc.vector.memset(warm[:], 0.0)
        warm2 = const.tile([P, 1], F32, name="warm2")
        nc.scalar.activation(out=warm2[:], in_=warm[:], func=TANH)

        dummy = const.tile([P, 512], BF16, name="dummy")
        nc.vector.memset(dummy[:], 0.0)
        for i in range(WARM_MATMULS):
            wz = ps_z.tile([P, 512], F32, name="z", tag="z")
            nc.tensor.matmul(wz[:], lhsT=dummy[:, :P], rhs=dummy[:], start=True, stop=True)

        ident = const.tile([P, P], F32, name="ident")
        make_identity(nc, ident[:])

        raw = []
        for n, (kind, i, width) in enumerate(SOURCES):
            x = xin.tile([P, 4 * width], BF16, name="x%d" % n)
            if kind == "w":
                w_ap = (W_comp, W_prot)[i[0]].rearrange("(p j) k -> p j k", j=4)
                if i[1] is not None:
                    w_ap = w_ap[:, 2 * i[1] : 2 * i[1] + 2, :]
                nc.sync.dma_start(out=x[:].rearrange("p (j k) -> p j k", k=D), in_=w_ap)
            elif kind == "c":
                src = comp_feat[i : i + width // LC].rearrange("b (p r) k -> p b (r k)", r=2)
                nc.sync.dma_start(out=x[:].rearrange("p (b f) -> p b f", f=2 * D), in_=src)
            else:
                src = prot_flat[i : i + width, :].rearrange("(t p) k -> p t k", p=P)
                nc.sync.dma_start(out=x[:].rearrange("p (t k) -> p t k", k=D), in_=src)
            raw.append(x)

        bias = []

        def cast_biases():
            for w in range(2):
                bt = const.tile([P, 4], F32, name="bias%d" % w)
                nc.vector.tensor_copy(out=bt[:], in_=bias_bf[w][:])
                bias.append(bt)

        def copy_out(engine, dst, src):
            if engine == "v":
                nc.vector.tensor_copy(out=dst, in_=src)
            else:
                nc.scalar.copy(out=dst, in_=src)

        xt_of, grouped, regrouped = {}, {}, {}
        x_q, t_q, w_q, comp_q = {}, {}, {}, {}
        z_of, th_of, o_of, out_tiles = {}, {}, {}, {}
        ramp_banks = []

        def tiles_of(n):
            return 2

        def banks_of(n):
            return range(SOURCES[n][2] // (P * tiles_of(n)))

        def transposes(n, banks=None):
            xf = raw[n][:].bitcast(F32)
            for h in banks_of(n):
                if banks is not None and banks[h] == "z":
                    xt = ps_z.tile([P, 512], F32, name="z", tag="z")
                elif (banks is None and n <= LAST_RAMP_SOURCE and len(ramp_banks) % 2 == 1) or (banks is not None and banks[h] == "o"):
                    xt = ps_o.tile([P, 512], F32, name="o", tag="o")
                else:
                    xt = ps_xt.tile([P, 512], F32, name="xt", tag="xt")
                ramp_banks.append(n)
                xt_of[(n, h)] = xt
                for tl in range(tiles_of(n)):
                    for u in range(2):
                        t = tiles_of(n) * h + tl
                        nc.tensor.transpose(
                            xt[:, (2 * tl + u) * P : (2 * tl + u + 1) * P],
                            xf[:, 256 * t + P * u : 256 * t + P * u + P],
                            ident[:],
                        )

        def place_of(n):
            if n not in grouped:
                xg = xgp.tile([P, 4 * SOURCES[n][2]], BF16, name="xg", tag="xg", align_bytes=64)
                grouped[n] = xg[:]
            return grouped[n]

        def copy_source(n, h, engine):
            xgf = place_of(n).bitcast(F32)
            nt = tiles_of(n)
            copy_out(
                engine,
                xgf[:, 256 * nt * h : 256 * nt * (h + 1)].rearrange("q (t a u) -> q t a u", t=nt, u=2),
                xt_of[(n, h)][:, : 256 * nt].rearrange("q (t u a) -> q t a u", t=nt, u=2),
            )

        def quantise_source(n):
            kind, i, width = SOURCES[n]
            if kind == "w":
                codes = const.tile([P, width], U32, name="wc%d" % n, align_bytes=64)
                scales = const.tile([P, width], U8, name="ws%d" % n, align_bytes=64)
                first_j = 0 if i[1] is None else 2 * i[1]
                for jj in range(width // P):
                    w_q[(i[0], first_j + jj)] = (codes[:, P * jj : P * jj + P], scales[:, P * jj : P * jj + P])
            else:
                codes = xqp.tile([P, width], U32, name="xc", tag="xc", align_bytes=64)
                scales = xqp.tile([P, width], U8, name="xs", tag="xs", align_bytes=64)
                x_q[n] = (codes[:], scales[:])
            nc.vector.quantize_mx(out=codes[:].bitcast(FP8X4), scales=scales[:], in_=grouped[n])

        def keep_trans(g, codes, scales):
            kind, i, width = SOURCES[GROUPS[g]]
            t_q[g] = (codes, scales)
            if kind == "c":
                for bb in range(width // LC):
                    comp_q[i + bb] = (codes, scales, LC * bb)

        def quantise_trans(g):
            kind, i, width = SOURCES[GROUPS[g]]
            pool = cq if kind == "c" else pq
            tcd = pool.tile([P, width], U32, name="tcd", tag="tcd", align_bytes=64)
            tsc = pool.tile([P, width], U8, name="tsc", tag="tsc", align_bytes=64)
            keep_trans(g, tcd[:], tsc[:])
            nc.vector.quantize_mx(out=tcd[:].bitcast(FP8X4), scales=tsc[:], in_=regrouped[g])

        def first_stage(g, js=range(4)):
            n = GROUPS[g]
            kind, i, width = SOURCES[n]
            xc, xs = x_q[n]
            for j in js:
                wc, ws = w_q[(0 if kind == "c" else 1, j)]
                z = ps_z.tile([P, 512], F32, name="z", tag="z")
                z_of[(g, j)] = z
                nc.tensor.matmul_mx(
                    out=z[:, :width],
                    lhsT=wc.bitcast(FP8X4),
                    lhsT_scale=ws,
                    rhs=xc.bitcast(FP8X4),
                    rhs_scale=xs,
                    start=True,
                    stop=True,
                )

        def tanh(g):
            kind, i, width = SOURCES[GROUPS[g]]
            th = tp.tile([P, 4 * width], BF16, name="th", tag="th")
            th_of[g] = th
            for j in range(4):
                nc.scalar.activation(
                    out=th[:, width * j : width * j + width],
                    in_=z_of[(g, j)][:, :width],
                    func=TANH,
                    bias=bias[0 if kind == "c" else 1][:, j : j + 1],
                    scale=1.0,
                )

        def regroup(g):
            width = SOURCES[GROUPS[g]][2]
            gr = gp.tile([P, 4 * width], BF16, name="gr", tag="gr", align_bytes=64)
            regrouped[g] = gr[:]
            nc.vector.tensor_copy(
                out=regrouped[g].rearrange("p (c i j) -> p c j i", i=2, j=4),
                in_=th_of[g][:].rearrange("p (j c i) -> p c j i", j=4, i=2),
            )

        def second_stage(g, wide=False):
            p_codes, p_scales = t_q[g]
            for un, (b, rs, c0, width, n0) in enumerate(units_of(g)):
                c_codes, c_scales, off = comp_q[b]
                if wide:
                    o = ps_xt.tile([P, 512], F32, name="xt", tag="xt")
                else:
                    o = ps_o.tile([P, 512], F32, name="o", tag="o")
                o_of[(g, un)] = o
                for q, r in enumerate(rs):
                    m0 = off + P * r
                    nc.tensor.matmul_mx(
                        out=o[:, q * width : (q + 1) * width],
                        lhsT=c_codes[:, m0 : m0 + P].bitcast(FP8X4),
                        lhsT_scale=c_scales[:, m0 : m0 + P],
                        rhs=p_codes[:, c0 : c0 + width].bitcast(FP8X4),
                        rhs_scale=p_scales[:, c0 : c0 + width],
                        start=True,
                        stop=True,
                    )

        def store(b, r0, r1, n0, n1):
            nc.sync.dma_start(
                out=out[b].rearrange("(a r) n -> a r n", r=2)[:, r0:r1, n0:n1],
                in_=out_tiles[b][:].rearrange("p (r n) -> p r n", r=2)[:, r0:r1, n0:n1],
            )

        def affinity_out(g, un, engine):
            b, rs, c0, width, n0 = units_of(g)[un]
            if b not in out_tiles:
                ot_new = op.tile([P, 2 * LP], F32, name="ot", tag="ot")
                out_tiles[b] = ot_new
            ot = out_tiles[b]
            o = o_of[(g, un)]
            if len(rs) == 1:
                copy_out(engine, ot[:, LP * rs[0] + n0 : LP * rs[0] + n0 + width], o[:, :width])
            else:
                copy_out(
                    engine,
                    ot[:].rearrange("p (r n) -> p r n", r=2)[:, :, n0 : n0 + width],
                    o[:, : 2 * width].rearrange("p (r n) -> p r n", r=2),
                )
            if g > LAST_FULL_STORE_GROUP:
                store(b, rs[0], rs[-1] + 1, n0, n0 + width)

        def full_stores(g):
            for b in range(B):
                if g <= LAST_FULL_STORE_GROUP and any(u[0] == b and u[4] + u[3] == LP for u in units_of(g)):
                    store(b, 0, 2, 0, LP)

        transposes(0, "x")
        transposes(1, "o")
        transposes(2, "z")
        transposes(3, "z")
        transposes(4, "xo")
        copy_source(0, 0, "v")
        copy_source(1, 0, "s")
        quantise_source(0)
        copy_source(2, 0, "v")
        quantise_source(1)
        copy_source(3, 0, "s")
        quantise_source(2)
        first_stage(0)
        cast_biases()
        quantise_source(3)
        copy_source(4, 0, "s")
        copy_source(4, 1, "v")
        tanh(0)
        transposes(5, "xo")
        first_stage(1)
        quantise_source(4)
        copy_source(5, 0, "v")
        copy_source(5, 1, "s")
        tanh(1)
        regroup(0)
        quantise_source(5)
        transposes(6, "xo")
        first_stage(2)
        quantise_trans(0)
        copy_source(6, 0, "v")
        copy_source(6, 1, "s")
        tanh(2)
        regroup(1)
        quantise_source(6)
        copied = []
        next_source = 7

        for s in range(2, LAST_LOOP_STEP + 1):
            new = []
            target = GROUPS[min(N_GROUPS - 1, s + LEAD)]
            while next_source <= target and len(new) < 2:
                new.append(next_source)
                next_source += 1
            g2 = s - 2
            n_units = len(units_of(g2))
            for n in new:
                transposes(n)
            if s > 2:
                regroup(s - 1)
            if n_units:
                second_stage(g2)
            first_stage(s + 1)
            if s > 2:
                tanh(s)
            for engine in "vs":
                for n in new:
                    for h in banks_of(n):
                        if ("s" if (s <= LAST_SCALAR_B_STEP and h == 1) else "v") == engine:
                            copy_source(n, h, engine)
            for un in range(n_units):
                if (g2, un) != (12, 0):
                    affinity_out(g2, un, "v" if (g2 in EXTRA and un == 0) else "s")
            if g2 != 12:
                full_stores(g2)
            quantise_trans(s - 1)
            for n in copied:
                quantise_source(n)
            copied = list(new)

        affinity_out(12, 0, "v")
        second_stage(13, True)
        first_stage(16)
        regroup(14)
        quantise_source(copied[0])
        quantise_trans(14)
        full_stores(12)
        tanh(15)
        affinity_out(13, 0, "v")
        affinity_out(13, 1, "s")
        full_stores(13)
        tanh(16)
        second_stage(14)
        first_stage(17)
        tanh(17)
        regroup(15)
        quantise_trans(15)
        regroup(16)
        second_stage(15, True)
        regroup(17)
        affinity_out(14, 0, "s")
        affinity_out(14, 1, "s")
        quantise_trans(16)
        quantise_trans(17)
        affinity_out(15, 0, "s")
        affinity_out(15, 1, "s")
        second_stage(16)
        second_stage(17, True)
        affinity_out(16, 0, "v")
        affinity_out(16, 1, "s")
        affinity_out(17, 0, "v")
        affinity_out(17, 1, "s")
